import numpy as np
import ml_dtypes


def mxq(x, axis, fmt="e4m3"):
    dtype, down = {"e4m3": (ml_dtypes.float8_e4m3fn, 7), "e5m2": (ml_dtypes.float8_e5m2, 14)}[fmt]
    v = np.moveaxis(np.asarray(x, np.float32).astype(ml_dtypes.bfloat16).astype(np.float64), axis, -1)
    blocks = v.reshape(v.shape[:-1] + (-1, 32))
    amax = np.abs(blocks).max(-1, keepdims=True)
    byte = np.maximum(np.where(amax > 0, np.frexp(amax)[1] - 1 + 127, 0) - down, 1)
    scale = np.exp2(byte - 127.0)
    codes = (blocks / scale).astype(np.float32).astype(dtype).astype(np.float64)
    return np.moveaxis((codes * scale).reshape(v.shape), -1, axis)


WIDE = False


def mx_kscale(k):
    if not WIDE:
        return np.ones(k)
    levels = np.array([10, -10, 5, -5, 0])
    a = np.random.permutation(np.resize(levels, k // 512 * 4)).reshape(k // 512, 4)
    idx = np.arange(k)
    return np.exp2(a[idx // 512, idx % 128 // 32])


BF16 = ml_dtypes.bfloat16


def bf(x):
    return np.asarray(x, np.float32).astype(BF16)


def f64(x):
    return np.asarray(x).astype(np.float64)


B, IN, OUT, N = 16384, 128, 128, 16
K = IN * N
MXB = 32


def chebyshev_basis(x, n):
    Ts = [np.ones_like(x), x]
    for _ in range(n - 2):
        Ts.append(2.0 * x * Ts[-1] - Ts[-2])
    return np.stack(Ts[:n], axis=-1)


def setup_inputs():
    wm = 2.0 / np.sqrt(K)
    x = np.random.uniform(-1.0, 1.0, (B, IN))
    w = np.random.uniform(-wm, wm, (OUT, IN, N))
    sb = np.repeat(mx_kscale(K)[::MXB], MXB // N)
    t = (sb / sb.min()) ** 2
    y = (np.log(2.0 * t) + np.abs(x)) / (N - 1)
    x = np.where(t > 1.0, np.sign(x) * np.cosh(y), x)
    return {"x": bf(x), "w": bf(w / t[:, None])}


def reference(x, w):
    x, w = f64(x), f64(w)
    basis = chebyshev_basis(x, w.shape[-1])
    bq = mxq(basis.reshape(x.shape[0], -1), 1, "e4m3")
    wq = mxq(w.reshape(w.shape[0], -1), 1, "e4m3")
    return bq @ wq.T

@@ -1,0 +1,210 @@
+from contextlib import ExitStack
+
+import concourse.mybir as mybir
+from concourse.masks import make_identity
+
+F32 = mybir.dt.float32
+BF16 = mybir.dt.bfloat16
+U32 = mybir.dt.uint32
+U8 = mybir.dt.uint8
+FP8X4 = mybir.dt.float8_e4m3fn_x4
+ALU = mybir.AluOpType
+ACT = mybir.ActivationFunctionType
+
+P = 128
+PACK = 4
+BATCH, FEATURES, OUTPUTS, DEGREES = 16384, 128, 128, 16
+PASSES = DEGREES // PACK
+
+WORD_DEGREES = ((0, 2, 4, 8), (1, 3, 5, 7), (6, 10, 12, 14), (9, 11, 13, 15))
+EVEN_LOW, ODD_LOW, EVEN_HIGH, ODD_HIGH = 0, 1, 2, 3
+
+CHUNK = 512
+TILES = CHUNK // P
+LOAD_ROWS = 16
+CHUNKS_PER_LOAD = LOAD_ROWS // TILES
+LOADS = BATCH // (P * LOAD_ROWS)
+RUN = 4
+DEPTH = 2
+
+FLOPS = 2 * BATCH * FEATURES * DEGREES * OUTPUTS
+
+
+def planes_in_word_order(planes):
+    return planes.rearrange("p t (c i) -> p c t i", i=RUN)
+
+
+def words_in_the_same_order(grouped):
+    return grouped.rearrange("p (c i) t -> p c t i", i=RUN)
+
+
+def quantise_weights(tc, keep, identity, w):
+    nc = tc.nc
+    w_codes = keep.tile([P, PASSES, OUTPUTS], U32, align_bytes=64)
+    w_scales = keep.tile([P, PASSES, OUTPUTS], U8, align_bytes=64)
+    with tc.tile_pool(name="w_stage", bufs=1) as stage, tc.psum_pool(name="w_psum", bufs=2) as psum:
+        w_rows = stage.tile([P, FEATURES * DEGREES], BF16)
+        nc.sync.dma_start(out=w_rows[:], in_=w.rearrange("o i n -> o (i n)"))
+        by_degree = w_rows[:].rearrange("o (g s q e n) -> o n g q s e", g=4, s=4, q=4, e=2)
+        w_sorted = stage.tile([P, DEGREES, FEATURES], BF16)
+        w_grouped = stage.tile([P, PASSES, OUTPUTS, PACK], BF16, align_bytes=64)
+        planes_per_bank = 2 * PACK
+        for first_pass in range(0, PASSES, 2):
+            w_turned = psum.tile([P, planes_per_bank, OUTPUTS], BF16)
+            for k in range(planes_per_bank):
+                degree = WORD_DEGREES[first_pass + k // PACK][k % PACK]
+                plane = w_sorted[:, first_pass * PACK + k, :]
+                nc.vector.tensor_copy(
+                    out=plane.rearrange("o (g q s e) -> o g q s e", g=4, q=4, s=4),
+                    in_=by_degree[:, degree],
+                )
+                nc.tensor.transpose(w_turned[:, k, :], plane, identity)
+            nc.vector.tensor_copy(
+                out=w_grouped[:, first_pass : first_pass + 2, :, :],
+                in_=w_turned[:].rearrange("p (c t) o -> p c o t", t=PACK),
+            )
+        nc.vector.quantize_mx(
+            out=w_codes[:].rearrange("p c o -> p (c o)").bitcast(FP8X4),
+            scales=w_scales[:].rearrange("p c o -> p (c o)"),
+            in_=w_grouped[:].rearrange("p c o t -> p (c o t)"),
+        )
+    return w_codes, w_scales
+
+
+def tile_function_kernel(tc, x, w, out):
+    nc = tc.nc
+
+    def square(out_plane, in_plane, scale, bias=None):
+        if bias is None:
+            nc.scalar.activation(out=out_plane, in_=in_plane, func=ACT.Square, scale=scale)
+        else:
+            nc.scalar.activation(out=out_plane, in_=in_plane, func=ACT.Square, scale=scale, bias=bias)
+
+    def shifted_product(out_plane, a, shift, b):
+        nc.vector.scalar_tensor_tensor(
+            out=out_plane, in0=a, scalar=shift, in1=b, op0=ALU.subtract, op1=ALU.mult
+        )
+
+    def subtract(out_plane, a, b):
+        nc.vector.tensor_tensor(out=out_plane, in0=a, in1=b, op=ALU.subtract)
+
+    with ExitStack() as ctx:
+        keep = ctx.enter_context(tc.tile_pool(name="keep", bufs=1))
+        identity = keep.tile([P, P], BF16)
+        make_identity(nc, identity[:])
+        minus_one = keep.tile([P, 1], F32)
+        minus_two = keep.tile([P, 1], F32)
+        minus_five_halves = keep.tile([P, 1], F32)
+        nc.vector.memset(minus_one[:], -1.0)
+        nc.vector.memset(minus_two[:], -2.0)
+        nc.vector.memset(minus_five_halves[:], -2.5)
+        even_low_tiles = []
+        for k in range(DEPTH):
+            fixed = keep.tile([P, PACK, CHUNK], F32, name="even_low_%d" % k)
+            nc.vector.memset(fixed[:, 0, :], 4.0)
+            even_low_tiles.append(fixed)
+
+        w_codes, w_scales = quantise_weights(tc, keep, identity[:], w)
+
+        loads = ctx.enter_context(tc.tile_pool(name="loads", bufs=2))
+        planes = ctx.enter_context(tc.tile_pool(name="planes", bufs=DEPTH))
+        words = ctx.enter_context(tc.tile_pool(name="words", bufs=DEPTH))
+        results = ctx.enter_context(tc.tile_pool(name="results", bufs=3))
+        x_psum = ctx.enter_context(tc.psum_pool(name="x_psum", bufs=2))
+        out_psum = ctx.enter_context(tc.psum_pool(name="out_psum", bufs=2))
+
+        x_loads = x.rearrange("(l p r) f -> l p (r f)", p=P, r=LOAD_ROWS)
+        out_loads = out.rearrange("(l p r) o -> l p r o", p=P, r=LOAD_ROWS)
+
+        for load in range(LOADS):
+            x_rows = loads.tile([P, LOAD_ROWS * FEATURES], BF16)
+            nc.sync.dma_start(out=x_rows[:], in_=x_loads[load])
+            x_sorted = loads.tile([P, LOAD_ROWS * FEATURES], BF16)
+            nc.vector.tensor_copy(
+                out=x_sorted[:].bitcast(F32).rearrange("p (a q s) -> p a q s", q=4, s=4),
+                in_=x_rows[:].bitcast(F32).rearrange("p (a s q) -> p a q s", q=4, s=4),
+            )
+
+            for part in range(CHUNKS_PER_LOAD):
+                first_row = part * TILES
+                x_turned = x_psum.tile([P, CHUNK], BF16)
+                for r in range(TILES):
+                    nc.tensor.transpose(
+                        x_turned[:, r * P : (r + 1) * P],
+                        x_sorted[:, (first_row + r) * FEATURES : (first_row + r + 1) * FEATURES],
+                        identity[:],
+                    )
+
+                even_low = even_low_tiles[(load * CHUNKS_PER_LOAD + part) % DEPTH]
+                odd_low = planes.tile([P, PACK, CHUNK], F32)
+                even_high = planes.tile([P, PACK, CHUNK], F32)
+                odd_high = planes.tile([P, PACK, CHUNK], F32)
+                s1, s2, s4 = even_low[:, 1, :], even_low[:, 2, :], even_low[:, 3, :]
+                t1, t3, t5, t7 = (odd_low[:, t, :] for t in range(PACK))
+                s3, s5, s6, s7 = (even_high[:, t, :] for t in range(PACK))
+                t9, t11, t13, t15 = (odd_high[:, t, :] for t in range(PACK))
+                five = planes.tile([P, CHUNK], F32)
+
+                nc.scalar.copy(out=t1, in_=x_turned[:])
+                square(s1, x_turned[:], 2.0)
+                square(s2, s1, 1.0, minus_two[:])
+                square(five[:], s1, 1.0, minus_five_halves[:])
+                square(s4, s2, 1.0, minus_two[:])
+                shifted_product(t3, s1, 3.0, t1)
+                shifted_product(t5, five[:], 1.25, t1)
+                shifted_product(t7, s2, 2.0, t3)
+                square(s3, t3, 2.0)
+                square(s5, t5, 2.0)
+                subtract(t7, t7, t1)
+                square(s6, s3, 1.0, minus_two[:])
+                square(s7, t7, 2.0)
+                shifted_product(t9, s3, 3.0, t3)
+                shifted_product(t11, s3, 2.0, t5)
+                shifted_product(t13, s3, 2.0, t7)
+                shifted_product(t15, s5, 3.0, t5)
+                subtract(t11, t11, t1)
+                subtract(t13, t13, t1)
+
+                codes = words.tile([P, PASSES, CHUNK], U32, align_bytes=64)
+                scales = words.tile([P, PASSES, CHUNK], U8, align_bytes=64)
+                grouped = {}
+                for c in range(PASSES):
+                    grouped[c] = words.tile([P, CHUNK, PACK], BF16, name="grouped_%d" % c, align_bytes=64)
+                for c, squares in ((EVEN_LOW, even_low), (EVEN_HIGH, even_high)):
+                    nc.scalar.activation(
+                        out=words_in_the_same_order(grouped[c][:]),
+                        in_=planes_in_word_order(squares[:]),
+                        func=ACT.Identity,
+                        scale=0.5,
+                        bias=minus_one[:],
+                    )
+                for c, values in ((ODD_LOW, odd_low), (ODD_HIGH, odd_high)):
+                    nc.vector.tensor_copy(
+                        out=words_in_the_same_order(grouped[c][:]),
+                        in_=planes_in_word_order(values[:]),
+                    )
+                for c in range(PASSES):
+                    nc.vector.quantize_mx(
+                        out=codes[:, c, :].bitcast(FP8X4),
+                        scales=scales[:, c, :],
+                        in_=grouped[c][:].rearrange("p w t -> p (w t)"),
+                    )
+
+                sums = out_psum.tile([P, TILES, OUTPUTS], F32)
+                for r in range(TILES):
+                    columns = slice(r * P, (r + 1) * P)
+                    for c in range(PASSES):
+                        nc.tensor.matmul_mx(
+                            out=sums[:, r, :],
+                            lhsT=codes[:, c, columns].bitcast(FP8X4),
+                            lhsT_scale=scales[:, c, columns],
+                            rhs=w_codes[:, c, :].bitcast(FP8X4),
+                            rhs_scale=w_scales[:, c, :],
+                            start=(c == 0),
+                            stop=(c == PASSES - 1),
+                        )
+                result = results.tile([P, TILES, OUTPUTS], F32)
+                nc.scalar.copy(out=result[:], in_=sums[:])
+                nc.scalar.dma_start(
+                    out=out_loads[load][:, first_row : first_row + TILES, :], in_=result[:]
+                )

@@ -16,7 +16,7 @@ PACK = 4
 BATCH, FEATURES, OUTPUTS, DEGREES = 16384, 128, 128, 16
 PASSES = DEGREES // PACK
 
-WORD_DEGREES = ((0, 2, 4, 8), (1, 3, 5, 7), (6, 10, 12, 14), (9, 11, 13, 15))
+WORD_DEGREES = ((0, 2, 4, 8), (1, 3, 5, 7), (6, 10, 14, 12), (9, 15, 11, 13))
 EVEN_LOW, ODD_LOW, EVEN_HIGH, ODD_HIGH = 0, 1, 2, 3
 
 CHUNK = 512
@@ -24,8 +24,9 @@ TILES = CHUNK // P
 LOAD_ROWS = 16
 CHUNKS_PER_LOAD = LOAD_ROWS // TILES
 LOADS = BATCH // (P * LOAD_ROWS)
+CHUNKS = BATCH // CHUNK
 RUN = 4
-DEPTH = 2
+VECTOR_COLUMNS = CHUNK - 5 * CHUNK // 16
 
 FLOPS = 2 * BATCH * FEATURES * DEGREES * OUTPUTS
 
@@ -98,113 +99,178 @@ def tile_function_kernel(tc, x, w, out):
         nc.vector.memset(minus_one[:], -1.0)
         nc.vector.memset(minus_two[:], -2.0)
         nc.vector.memset(minus_five_halves[:], -2.5)
-        even_low_tiles = []
-        for k in range(DEPTH):
-            fixed = keep.tile([P, PACK, CHUNK], F32, name="even_low_%d" % k)
-            nc.vector.memset(fixed[:, 0, :], 4.0)
-            even_low_tiles.append(fixed)
+        even_low_words = []
+        for k in range(2):
+            fixed = keep.tile([P, CHUNK, PACK], BF16, name="even_low_words_%d" % k, align_bytes=64)
+            nc.gpsimd.memset(fixed[:], 1.0)
+            even_low_words.append(fixed)
 
         w_codes, w_scales = quantise_weights(tc, keep, identity[:], w)
 
         loads = ctx.enter_context(tc.tile_pool(name="loads", bufs=2))
-        planes = ctx.enter_context(tc.tile_pool(name="planes", bufs=DEPTH))
-        words = ctx.enter_context(tc.tile_pool(name="words", bufs=DEPTH))
-        results = ctx.enter_context(tc.tile_pool(name="results", bufs=3))
+        three_rounds = ctx.enter_context(tc.tile_pool(name="three_rounds", bufs=3))
+        two_rounds = ctx.enter_context(tc.tile_pool(name="two_rounds", bufs=2))
         x_psum = ctx.enter_context(tc.psum_pool(name="x_psum", bufs=2))
         out_psum = ctx.enter_context(tc.psum_pool(name="out_psum", bufs=2))
 
         x_loads = x.rearrange("(l p r) f -> l p (r f)", p=P, r=LOAD_ROWS)
         out_loads = out.rearrange("(l p r) o -> l p r o", p=P, r=LOAD_ROWS)
 
-        for load in range(LOADS):
-            x_rows = loads.tile([P, LOAD_ROWS * FEATURES], BF16)
-            nc.sync.dma_start(out=x_rows[:], in_=x_loads[load])
-            x_sorted = loads.tile([P, LOAD_ROWS * FEATURES], BF16)
+        x_rows, x_sorted, x_turned = {}, {}, {}
+        even_low, odd_low, even_high, odd_high, five = {}, {}, {}, {}, {}
+        grouped, codes, scales, sums = {}, {}, {}, {}
+
+        def fetch(load):
+            x_rows[load] = loads.tile([P, LOAD_ROWS * FEATURES], BF16, name="x_rows")
+            nc.sync.dma_start(out=x_rows[load][:], in_=x_loads[load])
+
+        def sort_features(load):
+            x_sorted[load] = loads.tile([P, LOAD_ROWS * FEATURES], BF16, name="x_sorted")
             nc.vector.tensor_copy(
-                out=x_sorted[:].bitcast(F32).rearrange("p (a q s) -> p a q s", q=4, s=4),
-                in_=x_rows[:].bitcast(F32).rearrange("p (a s q) -> p a q s", q=4, s=4),
+                out=x_sorted[load][:].bitcast(F32).rearrange("p (a q s) -> p a q s", q=4, s=4),
+                in_=x_rows[load][:].bitcast(F32).rearrange("p (a s q) -> p a q s", q=4, s=4),
             )
 
-            for part in range(CHUNKS_PER_LOAD):
-                first_row = part * TILES
-                x_turned = x_psum.tile([P, CHUNK], BF16)
-                for r in range(TILES):
-                    nc.tensor.transpose(
-                        x_turned[:, r * P : (r + 1) * P],
-                        x_sorted[:, (first_row + r) * FEATURES : (first_row + r + 1) * FEATURES],
-                        identity[:],
-                    )
-
-                even_low = even_low_tiles[(load * CHUNKS_PER_LOAD + part) % DEPTH]
-                odd_low = planes.tile([P, PACK, CHUNK], F32)
-                even_high = planes.tile([P, PACK, CHUNK], F32)
-                odd_high = planes.tile([P, PACK, CHUNK], F32)
-                s1, s2, s4 = even_low[:, 1, :], even_low[:, 2, :], even_low[:, 3, :]
-                t1, t3, t5, t7 = (odd_low[:, t, :] for t in range(PACK))
-                s3, s5, s6, s7 = (even_high[:, t, :] for t in range(PACK))
-                t9, t11, t13, t15 = (odd_high[:, t, :] for t in range(PACK))
-                five = planes.tile([P, CHUNK], F32)
-
-                nc.scalar.copy(out=t1, in_=x_turned[:])
-                square(s1, x_turned[:], 2.0)
-                square(s2, s1, 1.0, minus_two[:])
-                square(five[:], s1, 1.0, minus_five_halves[:])
-                square(s4, s2, 1.0, minus_two[:])
-                shifted_product(t3, s1, 3.0, t1)
-                shifted_product(t5, five[:], 1.25, t1)
-                shifted_product(t7, s2, 2.0, t3)
-                square(s3, t3, 2.0)
-                square(s5, t5, 2.0)
-                subtract(t7, t7, t1)
-                square(s6, s3, 1.0, minus_two[:])
-                square(s7, t7, 2.0)
-                shifted_product(t9, s3, 3.0, t3)
-                shifted_product(t11, s3, 2.0, t5)
-                shifted_product(t13, s3, 2.0, t7)
-                shifted_product(t15, s5, 3.0, t5)
-                subtract(t11, t11, t1)
-                subtract(t13, t13, t1)
-
-                codes = words.tile([P, PASSES, CHUNK], U32, align_bytes=64)
-                scales = words.tile([P, PASSES, CHUNK], U8, align_bytes=64)
-                grouped = {}
-                for c in range(PASSES):
-                    grouped[c] = words.tile([P, CHUNK, PACK], BF16, name="grouped_%d" % c, align_bytes=64)
-                for c, squares in ((EVEN_LOW, even_low), (EVEN_HIGH, even_high)):
-                    nc.scalar.activation(
-                        out=words_in_the_same_order(grouped[c][:]),
-                        in_=planes_in_word_order(squares[:]),
-                        func=ACT.Identity,
-                        scale=0.5,
-                        bias=minus_one[:],
-                    )
-                for c, values in ((ODD_LOW, odd_low), (ODD_HIGH, odd_high)):
-                    nc.vector.tensor_copy(
-                        out=words_in_the_same_order(grouped[c][:]),
-                        in_=planes_in_word_order(values[:]),
-                    )
-                for c in range(PASSES):
-                    nc.vector.quantize_mx(
-                        out=codes[:, c, :].bitcast(FP8X4),
-                        scales=scales[:, c, :],
-                        in_=grouped[c][:].rearrange("p w t -> p (w t)"),
-                    )
-
-                sums = out_psum.tile([P, TILES, OUTPUTS], F32)
-                for r in range(TILES):
-                    columns = slice(r * P, (r + 1) * P)
-                    for c in range(PASSES):
-                        nc.tensor.matmul_mx(
-                            out=sums[:, r, :],
-                            lhsT=codes[:, c, columns].bitcast(FP8X4),
-                            lhsT_scale=scales[:, c, columns],
-                            rhs=w_codes[:, c, :].bitcast(FP8X4),
-                            rhs_scale=w_scales[:, c, :],
-                            start=(c == 0),
-                            stop=(c == PASSES - 1),
-                        )
-                result = results.tile([P, TILES, OUTPUTS], F32)
-                nc.scalar.copy(out=result[:], in_=sums[:])
-                nc.scalar.dma_start(
-                    out=out_loads[load][:, first_row : first_row + TILES, :], in_=result[:]
+        def turn(k):
+            x_turned[k] = x_psum.tile([P, CHUNK], BF16, name="x_turned")
+            for r in range(TILES):
+                row = (k % CHUNKS_PER_LOAD) * TILES + r
+                nc.tensor.transpose(
+                    x_turned[k][:, r * P : (r + 1) * P],
+                    x_sorted[k // CHUNKS_PER_LOAD][:, row * FEATURES : (row + 1) * FEATURES],
+                    identity[:],
                 )
+
+        def squares_from_x(k):
+            even_low[k] = three_rounds.tile([P, PACK - 1, CHUNK], F32, name="even_low")
+            odd_low[k] = three_rounds.tile([P, PACK, CHUNK], F32, name="odd_low")
+            five[k] = two_rounds.tile([P, CHUNK], F32, name="five")
+            s1, s2, s4 = (even_low[k][:, t, :] for t in range(PACK - 1))
+            square(s1, x_turned[k][:], 2.0)
+            nc.scalar.copy(out=odd_low[k][:, 0, :], in_=x_turned[k][:])
+            square(s2, s1, 1.0, minus_two[:])
+            square(five[k][:], s1, 1.0, minus_five_halves[:])
+            square(s4, s2, 1.0, minus_two[:])
+
+        def t3_t5_and_most_of_t7(k):
+            t1, t3, t5, t7 = (odd_low[k][:, t, :] for t in range(PACK))
+            shifted_product(t3, even_low[k][:, 0, :], 3.0, t1)
+            shifted_product(t5, five[k][:], 1.25, t1)
+            shifted_product(t7, even_low[k][:, 1, :], 2.0, t3)
+
+        def finish_t7(k):
+            subtract(odd_low[k][:, 3, :], odd_low[k][:, 3, :], odd_low[k][:, 0, :])
+
+        def squares_from_odd(k):
+            even_high[k] = two_rounds.tile([P, PACK, CHUNK], F32, name="even_high")
+            square(even_high[k][:, 0:2, :], odd_low[k][:, 1:3, :], 2.0)
+            square(even_high[k][:, 2, :], odd_low[k][:, 3, :], 2.0)
+            square(even_high[k][:, 3, :], even_high[k][:, 0, :], 1.0, minus_two[:])
+
+        def high_odd_degrees(k):
+            odd_high[k] = two_rounds.tile([P, PACK, CHUNK], F32, name="odd_high")
+            s3_twice = even_high[k][:, 0:1, :].to_broadcast([P, 2, CHUNK])
+            t1_twice = odd_low[k][:, 0:1, :].to_broadcast([P, 2, CHUNK])
+            shifted_product(odd_high[k][:, 2:4, :], s3_twice, 2.0, odd_low[k][:, 2:4, :])
+            shifted_product(odd_high[k][:, 0:2, :], even_high[k][:, 0:2, :], 3.0, odd_low[k][:, 1:3, :])
+            subtract(odd_high[k][:, 2:4, :], odd_high[k][:, 2:4, :], t1_twice)
+
+        def round_odd_low_on_vector(k):
+            grouped[k] = {EVEN_LOW: even_low_words[k % 2]}
+            grouped[k][ODD_LOW] = two_rounds.tile([P, CHUNK, PACK], BF16, name="odd_low_words", align_bytes=64)
+            nc.vector.tensor_copy(
+                out=words_in_the_same_order(grouped[k][ODD_LOW][:, :VECTOR_COLUMNS, :]),
+                in_=planes_in_word_order(odd_low[k][:, :, :VECTOR_COLUMNS]),
+            )
+
+        def round_odd_high(k):
+            grouped[k][ODD_HIGH] = two_rounds.tile([P, CHUNK, PACK], BF16, name="odd_high_words", align_bytes=64)
+            nc.vector.tensor_copy(
+                out=words_in_the_same_order(grouped[k][ODD_HIGH][:]),
+                in_=planes_in_word_order(odd_high[k][:]),
+            )
+
+        def round_on_scalar(k):
+            grouped[k][EVEN_HIGH] = two_rounds.tile([P, CHUNK, PACK], BF16, name="even_high_words", align_bytes=64)
+            for squares, word_values in (
+                (even_low[k][:], grouped[k][EVEN_LOW][:, :, 1:PACK]),
+                (even_high[k][:], grouped[k][EVEN_HIGH][:]),
+            ):
+                nc.scalar.activation(
+                    out=words_in_the_same_order(word_values),
+                    in_=planes_in_word_order(squares),
+                    func=ACT.Identity,
+                    scale=0.5,
+                    bias=minus_one[:],
+                )
+            nc.scalar.copy(
+                out=words_in_the_same_order(grouped[k][ODD_LOW][:, VECTOR_COLUMNS:, :]),
+                in_=planes_in_word_order(odd_low[k][:, :, VECTOR_COLUMNS:]),
+            )
+
+        def quantise(k):
+            codes[k] = two_rounds.tile([P, PASSES, CHUNK], U32, name="codes", align_bytes=64)
+            scales[k] = two_rounds.tile([P, PASSES, CHUNK], U8, name="scales", align_bytes=64)
+            for c in range(PASSES):
+                nc.vector.quantize_mx(
+                    out=codes[k][:, c, :].bitcast(FP8X4),
+                    scales=scales[k][:, c, :],
+                    in_=grouped[k][c][:].rearrange("p w t -> p (w t)"),
+                )
+
+        def multiply(k):
+            sums[k] = out_psum.tile([P, TILES, OUTPUTS], F32, name="sums")
+            for r in range(TILES):
+                columns = slice(r * P, (r + 1) * P)
+                for c in range(PASSES):
+                    nc.tensor.matmul_mx(
+                        out=sums[k][:, r, :],
+                        lhsT=codes[k][:, c, columns].bitcast(FP8X4),
+                        lhsT_scale=scales[k][:, c, columns],
+                        rhs=w_codes[:, c, :].bitcast(FP8X4),
+                        rhs_scale=w_scales[:, c, :],
+                        start=(c == 0),
+                        stop=(c == PASSES - 1),
+                    )
+
+        def store(k):
+            result = three_rounds.tile([P, TILES, OUTPUTS], F32, name="result")
+            nc.scalar.copy(out=result[:], in_=sums[k][:])
+            first_row = (k % CHUNKS_PER_LOAD) * TILES
+            nc.scalar.dma_start(
+                out=out_loads[k // CHUNKS_PER_LOAD][:, first_row : first_row + TILES, :], in_=result[:]
+            )
+
+        def is_chunk(k):
+            return 0 <= k < CHUNKS
+
+        fetch(0)
+        with tc.manual_schedule():
+            for j in range(-2, CHUNKS + 3):
+                if is_chunk(j + 2):
+                    if (j + 2) % CHUNKS_PER_LOAD == 0:
+                        load = (j + 2) // CHUNKS_PER_LOAD
+                        if load + 1 < LOADS:
+                            fetch(load + 1)
+                        sort_features(load)
+                    turn(j + 2)
+                if is_chunk(j + 1):
+                    squares_from_x(j + 1)
+                if is_chunk(j):
+                    t3_t5_and_most_of_t7(j)
+                if is_chunk(j - 1):
+                    round_odd_low_on_vector(j - 1)
+                if is_chunk(j):
+                    finish_t7(j)
+                    squares_from_odd(j)
+                if is_chunk(j - 1):
+                    round_odd_high(j - 1)
+                if is_chunk(j - 2):
+                    quantise(j - 2)
+                    multiply(j - 2)
+                if is_chunk(j):
+                    high_odd_degrees(j)
+                if is_chunk(j - 1):
+                    round_on_scalar(j - 1)
+                if is_chunk(j - 3):
+                    store(j - 3)

@@ -26,7 +26,7 @@ CHUNKS_PER_LOAD = LOAD_ROWS // TILES
 LOADS = BATCH // (P * LOAD_ROWS)
 CHUNKS = BATCH // CHUNK
 RUN = 4
-VECTOR_COLUMNS = CHUNK - 5 * CHUNK // 16
+VECTOR_COLUMNS = CHUNK - 3 * CHUNK // 16
 
 FLOPS = 2 * BATCH * FEATURES * DEGREES * OUTPUTS
 
@@ -99,11 +99,11 @@ def tile_function_kernel(tc, x, w, out):
         nc.vector.memset(minus_one[:], -1.0)
         nc.vector.memset(minus_two[:], -2.0)
         nc.vector.memset(minus_five_halves[:], -2.5)
-        even_low_words = []
-        for k in range(2):
-            fixed = keep.tile([P, CHUNK, PACK], BF16, name="even_low_words_%d" % k, align_bytes=64)
-            nc.gpsimd.memset(fixed[:], 1.0)
-            even_low_words.append(fixed)
+        even_low_planes = []
+        for k in range(3):
+            fixed = keep.tile([P, PACK, CHUNK], F32, name="even_low_planes_%d" % k)
+            nc.gpsimd.memset(fixed[:, 0, :], 4.0)
+            even_low_planes.append(fixed)
 
         w_codes, w_scales = quantise_weights(tc, keep, identity[:], w)
 
@@ -142,10 +142,10 @@ def tile_function_kernel(tc, x, w, out):
                 )
 
         def squares_from_x(k):
-            even_low[k] = three_rounds.tile([P, PACK - 1, CHUNK], F32, name="even_low")
+            even_low[k] = even_low_planes[k % 3]
             odd_low[k] = three_rounds.tile([P, PACK, CHUNK], F32, name="odd_low")
             five[k] = two_rounds.tile([P, CHUNK], F32, name="five")
-            s1, s2, s4 = (even_low[k][:, t, :] for t in range(PACK - 1))
+            s1, s2, s4 = (even_low[k][:, t, :] for t in range(1, PACK))
             square(s1, x_turned[k][:], 2.0)
             nc.scalar.copy(out=odd_low[k][:, 0, :], in_=x_turned[k][:])
             square(s2, s1, 1.0, minus_two[:])
@@ -154,9 +154,9 @@ def tile_function_kernel(tc, x, w, out):
 
         def t3_t5_and_most_of_t7(k):
             t1, t3, t5, t7 = (odd_low[k][:, t, :] for t in range(PACK))
-            shifted_product(t3, even_low[k][:, 0, :], 3.0, t1)
+            shifted_product(t3, even_low[k][:, 1, :], 3.0, t1)
             shifted_product(t5, five[k][:], 1.25, t1)
-            shifted_product(t7, even_low[k][:, 1, :], 2.0, t3)
+            shifted_product(t7, even_low[k][:, 2, :], 2.0, t3)
 
         def finish_t7(k):
             subtract(odd_low[k][:, 3, :], odd_low[k][:, 3, :], odd_low[k][:, 0, :])
@@ -176,7 +176,7 @@ def tile_function_kernel(tc, x, w, out):
             subtract(odd_high[k][:, 2:4, :], odd_high[k][:, 2:4, :], t1_twice)
 
         def round_odd_low_on_vector(k):
-            grouped[k] = {EVEN_LOW: even_low_words[k % 2]}
+            grouped[k] = {}
             grouped[k][ODD_LOW] = two_rounds.tile([P, CHUNK, PACK], BF16, name="odd_low_words", align_bytes=64)
             nc.vector.tensor_copy(
                 out=words_in_the_same_order(grouped[k][ODD_LOW][:, :VECTOR_COLUMNS, :]),
@@ -191,14 +191,12 @@ def tile_function_kernel(tc, x, w, out):
             )
 
         def round_on_scalar(k):
+            grouped[k][EVEN_LOW] = two_rounds.tile([P, CHUNK, PACK], BF16, name="even_low_words", align_bytes=64)
             grouped[k][EVEN_HIGH] = two_rounds.tile([P, CHUNK, PACK], BF16, name="even_high_words", align_bytes=64)
-            for squares, word_values in (
-                (even_low[k][:], grouped[k][EVEN_LOW][:, :, 1:PACK]),
-                (even_high[k][:], grouped[k][EVEN_HIGH][:]),
-            ):
+            for c, squares in ((EVEN_LOW, even_low[k]), (EVEN_HIGH, even_high[k])):
                 nc.scalar.activation(
-                    out=words_in_the_same_order(word_values),
-                    in_=planes_in_word_order(squares),
+                    out=words_in_the_same_order(grouped[k][c][:]),
+                    in_=planes_in_word_order(squares[:]),
                     func=ACT.Identity,
                     scale=0.5,
                     bias=minus_one[:],
@@ -237,7 +235,7 @@ def tile_function_kernel(tc, x, w, out):
             result = three_rounds.tile([P, TILES, OUTPUTS], F32, name="result")
             nc.scalar.copy(out=result[:], in_=sums[k][:])
             first_row = (k % CHUNKS_PER_LOAD) * TILES
-            nc.scalar.dma_start(
+            nc.sync.dma_start(
                 out=out_loads[k // CHUNKS_PER_LOAD][:, first_row : first_row + TILES, :], in_=result[:]
             )
 

@@ -26,7 +26,8 @@ CHUNKS_PER_LOAD = LOAD_ROWS // TILES
 LOADS = BATCH // (P * LOAD_ROWS)
 CHUNKS = BATCH // CHUNK
 RUN = 4
-VECTOR_COLUMNS = CHUNK - 3 * CHUNK // 16
+GPSIMD_COLUMNS = 3 * CHUNK // 4
+VECTOR_COLUMNS = 5 * CHUNK // 16
 
 FLOPS = 2 * BATCH * FEATURES * DEGREES * OUTPUTS
 
@@ -110,7 +111,8 @@ def tile_function_kernel(tc, x, w, out):
         loads = ctx.enter_context(tc.tile_pool(name="loads", bufs=2))
         three_rounds = ctx.enter_context(tc.tile_pool(name="three_rounds", bufs=3))
         two_rounds = ctx.enter_context(tc.tile_pool(name="two_rounds", bufs=2))
-        x_psum = ctx.enter_context(tc.psum_pool(name="x_psum", bufs=2))
+        four_rounds = ctx.enter_context(tc.tile_pool(name="four_rounds", bufs=4))
+        x_psum = ctx.enter_context(tc.psum_pool(name="x_psum", bufs=3))
         out_psum = ctx.enter_context(tc.psum_pool(name="out_psum", bufs=2))
 
         x_loads = x.rearrange("(l p r) f -> l p (r f)", p=P, r=LOAD_ROWS)
@@ -152,31 +154,45 @@ def tile_function_kernel(tc, x, w, out):
             square(five[k][:], s1, 1.0, minus_five_halves[:])
             square(s4, s2, 1.0, minus_two[:])
 
-        def t3_t5_and_most_of_t7(k):
-            t1, t3, t5, t7 = (odd_low[k][:, t, :] for t in range(PACK))
-            shifted_product(t3, even_low[k][:, 1, :], 3.0, t1)
-            shifted_product(t5, five[k][:], 1.25, t1)
-            shifted_product(t7, even_low[k][:, 2, :], 2.0, t3)
+        def round_even_low_on_gpsimd(k):
+            grouped[k] = {}
+            grouped[k][EVEN_LOW] = four_rounds.tile([P, CHUNK, PACK], BF16, name="even_low_words", align_bytes=64)
+            nc.gpsimd.tensor_scalar(
+                out=words_in_the_same_order(grouped[k][EVEN_LOW][:, :GPSIMD_COLUMNS, :]),
+                in0=planes_in_word_order(even_low[k][:, :, :GPSIMD_COLUMNS]),
+                scalar1=0.5,
+                scalar2=-1.0,
+                op0=ALU.mult,
+                op1=ALU.add,
+            )
+
+        def t5_and_t3(k):
+            shifted_product(odd_low[k][:, 2, :], five[k][:], 1.25, x_turned[k][:])
+            shifted_product(odd_low[k][:, 1, :], even_low[k][:, 1, :], 3.0, x_turned[k][:])
+
+        def most_of_t7(k):
+            shifted_product(odd_low[k][:, 3, :], even_low[k][:, 2, :], 2.0, odd_low[k][:, 1, :])
 
         def finish_t7(k):
             subtract(odd_low[k][:, 3, :], odd_low[k][:, 3, :], odd_low[k][:, 0, :])
 
-        def squares_from_odd(k):
+        def s3_and_s5(k):
             even_high[k] = two_rounds.tile([P, PACK, CHUNK], F32, name="even_high")
             square(even_high[k][:, 0:2, :], odd_low[k][:, 1:3, :], 2.0)
+
+        def s7_and_s6(k):
             square(even_high[k][:, 2, :], odd_low[k][:, 3, :], 2.0)
             square(even_high[k][:, 3, :], even_high[k][:, 0, :], 1.0, minus_two[:])
 
         def high_odd_degrees(k):
             odd_high[k] = two_rounds.tile([P, PACK, CHUNK], F32, name="odd_high")
             s3_twice = even_high[k][:, 0:1, :].to_broadcast([P, 2, CHUNK])
-            t1_twice = odd_low[k][:, 0:1, :].to_broadcast([P, 2, CHUNK])
+            x_twice = x_turned[k][:].unsqueeze(1).to_broadcast([P, 2, CHUNK])
             shifted_product(odd_high[k][:, 2:4, :], s3_twice, 2.0, odd_low[k][:, 2:4, :])
             shifted_product(odd_high[k][:, 0:2, :], even_high[k][:, 0:2, :], 3.0, odd_low[k][:, 1:3, :])
-            subtract(odd_high[k][:, 2:4, :], odd_high[k][:, 2:4, :], t1_twice)
+            subtract(odd_high[k][:, 2:4, :], odd_high[k][:, 2:4, :], x_twice)
 
         def round_odd_low_on_vector(k):
-            grouped[k] = {}
             grouped[k][ODD_LOW] = two_rounds.tile([P, CHUNK, PACK], BF16, name="odd_low_words", align_bytes=64)
             nc.vector.tensor_copy(
                 out=words_in_the_same_order(grouped[k][ODD_LOW][:, :VECTOR_COLUMNS, :]),
@@ -191,12 +207,11 @@ def tile_function_kernel(tc, x, w, out):
             )
 
         def round_on_scalar(k):
-            grouped[k][EVEN_LOW] = two_rounds.tile([P, CHUNK, PACK], BF16, name="even_low_words", align_bytes=64)
             grouped[k][EVEN_HIGH] = two_rounds.tile([P, CHUNK, PACK], BF16, name="even_high_words", align_bytes=64)
-            for c, squares in ((EVEN_LOW, even_low[k]), (EVEN_HIGH, even_high[k])):
+            for c, squares, first in ((EVEN_HIGH, even_high[k], 0), (EVEN_LOW, even_low[k], GPSIMD_COLUMNS)):
                 nc.scalar.activation(
-                    out=words_in_the_same_order(grouped[k][c][:]),
-                    in_=planes_in_word_order(squares[:]),
+                    out=words_in_the_same_order(grouped[k][c][:, first:, :]),
+                    in_=planes_in_word_order(squares[:, :, first:]),
                     func=ACT.Identity,
                     scale=0.5,
                     bias=minus_one[:],
@@ -245,6 +260,11 @@ def tile_function_kernel(tc, x, w, out):
         fetch(0)
         with tc.manual_schedule():
             for j in range(-2, CHUNKS + 3):
+                if is_chunk(j + 1):
+                    squares_from_x(j + 1)
+                    round_even_low_on_gpsimd(j + 1)
+                if is_chunk(j):
+                    t5_and_t3(j)
                 if is_chunk(j + 2):
                     if (j + 2) % CHUNKS_PER_LOAD == 0:
                         load = (j + 2) // CHUNKS_PER_LOAD
@@ -252,23 +272,22 @@ def tile_function_kernel(tc, x, w, out):
                             fetch(load + 1)
                         sort_features(load)
                     turn(j + 2)
-                if is_chunk(j + 1):
-                    squares_from_x(j + 1)
-                if is_chunk(j):
-                    t3_t5_and_most_of_t7(j)
                 if is_chunk(j - 1):
                     round_odd_low_on_vector(j - 1)
                 if is_chunk(j):
-                    finish_t7(j)
-                    squares_from_odd(j)
+                    most_of_t7(j)
+                    s3_and_s5(j)
                 if is_chunk(j - 1):
                     round_odd_high(j - 1)
+                if is_chunk(j):
+                    finish_t7(j)
                 if is_chunk(j - 2):
                     quantise(j - 2)
                     multiply(j - 2)
-                if is_chunk(j):
-                    high_odd_degrees(j)
                 if is_chunk(j - 1):
                     round_on_scalar(j - 1)
+                if is_chunk(j):
+                    s7_and_s6(j)
+                    high_odd_degrees(j)
                 if is_chunk(j - 3):
                     store(j - 3)

@@ -26,8 +26,7 @@ CHUNKS_PER_LOAD = LOAD_ROWS // TILES
 LOADS = BATCH // (P * LOAD_ROWS)
 CHUNKS = BATCH // CHUNK
 RUN = 4
-GPSIMD_COLUMNS = 3 * CHUNK // 4
-VECTOR_COLUMNS = 5 * CHUNK // 16
+VECTOR_COLUMNS = 3 * CHUNK // 16
 
 FLOPS = 2 * BATCH * FEATURES * DEGREES * OUTPUTS
 
@@ -44,7 +43,7 @@ def quantise_weights(tc, keep, identity, w):
     nc = tc.nc
     w_codes = keep.tile([P, PASSES, OUTPUTS], U32, align_bytes=64)
     w_scales = keep.tile([P, PASSES, OUTPUTS], U8, align_bytes=64)
-    with tc.tile_pool(name="w_stage", bufs=1) as stage, tc.psum_pool(name="w_psum", bufs=2) as psum:
+    with tc.tile_pool(name="w_stage", bufs=1) as stage, tc.psum_pool(name="w_psum", bufs=1) as psum:
         w_rows = stage.tile([P, FEATURES * DEGREES], BF16)
         nc.sync.dma_start(out=w_rows[:], in_=w.rearrange("o i n -> o (i n)"))
         by_degree = w_rows[:].rearrange("o (g s q e n) -> o n g q s e", g=4, s=4, q=4, e=2)
@@ -101,18 +100,16 @@ def tile_function_kernel(tc, x, w, out):
         nc.vector.memset(minus_two[:], -2.0)
         nc.vector.memset(minus_five_halves[:], -2.5)
         even_low_planes = []
-        for k in range(3):
+        for k in range(2):
             fixed = keep.tile([P, PACK, CHUNK], F32, name="even_low_planes_%d" % k)
             nc.gpsimd.memset(fixed[:, 0, :], 4.0)
             even_low_planes.append(fixed)
 
-        w_codes, w_scales = quantise_weights(tc, keep, identity[:], w)
-
         loads = ctx.enter_context(tc.tile_pool(name="loads", bufs=2))
         three_rounds = ctx.enter_context(tc.tile_pool(name="three_rounds", bufs=3))
         two_rounds = ctx.enter_context(tc.tile_pool(name="two_rounds", bufs=2))
-        four_rounds = ctx.enter_context(tc.tile_pool(name="four_rounds", bufs=4))
-        x_psum = ctx.enter_context(tc.psum_pool(name="x_psum", bufs=3))
+        five_rounds = ctx.enter_context(tc.tile_pool(name="five_rounds", bufs=5))
+        x_psum = ctx.enter_context(tc.psum_pool(name="x_psum", bufs=5))
         out_psum = ctx.enter_context(tc.psum_pool(name="out_psum", bufs=2))
 
         x_loads = x.rearrange("(l p r) f -> l p (r f)", p=P, r=LOAD_ROWS)
@@ -144,7 +141,7 @@ def tile_function_kernel(tc, x, w, out):
                 )
 
         def squares_from_x(k):
-            even_low[k] = even_low_planes[k % 3]
+            even_low[k] = even_low_planes[k % 2]
             odd_low[k] = three_rounds.tile([P, PACK, CHUNK], F32, name="odd_low")
             five[k] = two_rounds.tile([P, CHUNK], F32, name="five")
             s1, s2, s4 = (even_low[k][:, t, :] for t in range(1, PACK))
@@ -156,10 +153,10 @@ def tile_function_kernel(tc, x, w, out):
 
         def round_even_low_on_gpsimd(k):
             grouped[k] = {}
-            grouped[k][EVEN_LOW] = four_rounds.tile([P, CHUNK, PACK], BF16, name="even_low_words", align_bytes=64)
+            grouped[k][EVEN_LOW] = five_rounds.tile([P, CHUNK, PACK], BF16, name="even_low_words", align_bytes=64)
             nc.gpsimd.tensor_scalar(
-                out=words_in_the_same_order(grouped[k][EVEN_LOW][:, :GPSIMD_COLUMNS, :]),
-                in0=planes_in_word_order(even_low[k][:, :, :GPSIMD_COLUMNS]),
+                out=words_in_the_same_order(grouped[k][EVEN_LOW][:]),
+                in0=planes_in_word_order(even_low[k][:]),
                 scalar1=0.5,
                 scalar2=-1.0,
                 op0=ALU.mult,
@@ -174,7 +171,7 @@ def tile_function_kernel(tc, x, w, out):
             shifted_product(odd_low[k][:, 3, :], even_low[k][:, 2, :], 2.0, odd_low[k][:, 1, :])
 
         def finish_t7(k):
-            subtract(odd_low[k][:, 3, :], odd_low[k][:, 3, :], odd_low[k][:, 0, :])
+            subtract(odd_low[k][:, 3, :], odd_low[k][:, 3, :], x_turned[k][:])
 
         def s3_and_s5(k):
             even_high[k] = two_rounds.tile([P, PACK, CHUNK], F32, name="even_high")
@@ -184,16 +181,18 @@ def tile_function_kernel(tc, x, w, out):
             square(even_high[k][:, 2, :], odd_low[k][:, 3, :], 2.0)
             square(even_high[k][:, 3, :], even_high[k][:, 0, :], 1.0, minus_two[:])
 
-        def high_odd_degrees(k):
+        def high_odd_products(k):
             odd_high[k] = two_rounds.tile([P, PACK, CHUNK], F32, name="odd_high")
             s3_twice = even_high[k][:, 0:1, :].to_broadcast([P, 2, CHUNK])
-            x_twice = x_turned[k][:].unsqueeze(1).to_broadcast([P, 2, CHUNK])
             shifted_product(odd_high[k][:, 2:4, :], s3_twice, 2.0, odd_low[k][:, 2:4, :])
             shifted_product(odd_high[k][:, 0:2, :], even_high[k][:, 0:2, :], 3.0, odd_low[k][:, 1:3, :])
+
+        def finish_t11_and_t13(k):
+            x_twice = x_turned[k][:].unsqueeze(1).to_broadcast([P, 2, CHUNK])
             subtract(odd_high[k][:, 2:4, :], odd_high[k][:, 2:4, :], x_twice)
 
         def round_odd_low_on_vector(k):
-            grouped[k][ODD_LOW] = two_rounds.tile([P, CHUNK, PACK], BF16, name="odd_low_words", align_bytes=64)
+            grouped[k][ODD_LOW] = three_rounds.tile([P, CHUNK, PACK], BF16, name="odd_low_words", align_bytes=64)
             nc.vector.tensor_copy(
                 out=words_in_the_same_order(grouped[k][ODD_LOW][:, :VECTOR_COLUMNS, :]),
                 in_=planes_in_word_order(odd_low[k][:, :, :VECTOR_COLUMNS]),
@@ -207,15 +206,14 @@ def tile_function_kernel(tc, x, w, out):
             )
 
         def round_on_scalar(k):
-            grouped[k][EVEN_HIGH] = two_rounds.tile([P, CHUNK, PACK], BF16, name="even_high_words", align_bytes=64)
-            for c, squares, first in ((EVEN_HIGH, even_high[k], 0), (EVEN_LOW, even_low[k], GPSIMD_COLUMNS)):
-                nc.scalar.activation(
-                    out=words_in_the_same_order(grouped[k][c][:, first:, :]),
-                    in_=planes_in_word_order(squares[:, :, first:]),
-                    func=ACT.Identity,
-                    scale=0.5,
-                    bias=minus_one[:],
-                )
+            grouped[k][EVEN_HIGH] = three_rounds.tile([P, CHUNK, PACK], BF16, name="even_high_words", align_bytes=64)
+            nc.scalar.activation(
+                out=words_in_the_same_order(grouped[k][EVEN_HIGH][:]),
+                in_=planes_in_word_order(even_high[k][:]),
+                func=ACT.Identity,
+                scale=0.5,
+                bias=minus_one[:],
+            )
             nc.scalar.copy(
                 out=words_in_the_same_order(grouped[k][ODD_LOW][:, VECTOR_COLUMNS:, :]),
                 in_=planes_in_word_order(odd_low[k][:, :, VECTOR_COLUMNS:]),
@@ -259,35 +257,40 @@ def tile_function_kernel(tc, x, w, out):
 
         fetch(0)
         with tc.manual_schedule():
+            fetch(1)
+            sort_features(0)
+            turn(0)
+            w_codes, w_scales = quantise_weights(tc, keep, identity[:], w)
             for j in range(-2, CHUNKS + 3):
-                if is_chunk(j + 1):
-                    squares_from_x(j + 1)
-                    round_even_low_on_gpsimd(j + 1)
-                if is_chunk(j):
-                    t5_and_t3(j)
                 if is_chunk(j + 2):
-                    if (j + 2) % CHUNKS_PER_LOAD == 0:
-                        load = (j + 2) // CHUNKS_PER_LOAD
+                    squares_from_x(j + 2)
+                    round_even_low_on_gpsimd(j + 2)
+                if is_chunk(j - 1):
+                    finish_t11_and_t13(j - 1)
+                if is_chunk(j):
+                    finish_t7(j)
+                    s7_and_s6(j)
+                if is_chunk(j + 1):
+                    t5_and_t3(j + 1)
+                    s3_and_s5(j + 1)
+                if is_chunk(j + 3):
+                    if (j + 3) % CHUNKS_PER_LOAD == 0:
+                        load = (j + 3) // CHUNKS_PER_LOAD
                         if load + 1 < LOADS:
                             fetch(load + 1)
                         sort_features(load)
-                    turn(j + 2)
-                if is_chunk(j - 1):
-                    round_odd_low_on_vector(j - 1)
+                    turn(j + 3)
                 if is_chunk(j):
-                    most_of_t7(j)
-                    s3_and_s5(j)
+                    round_odd_low_on_vector(j)
+                    round_on_scalar(j)
+                if is_chunk(j + 1):
+                    most_of_t7(j + 1)
                 if is_chunk(j - 1):
                     round_odd_high(j - 1)
-                if is_chunk(j):
-                    finish_t7(j)
                 if is_chunk(j - 2):
                     quantise(j - 2)
                     multiply(j - 2)
-                if is_chunk(j - 1):
-                    round_on_scalar(j - 1)
                 if is_chunk(j):
-                    s7_and_s6(j)
-                    high_odd_degrees(j)
+                    high_odd_products(j)
                 if is_chunk(j - 3):
                     store(j - 3)

@@ -26,7 +26,7 @@ CHUNKS_PER_LOAD = LOAD_ROWS // TILES
 LOADS = BATCH // (P * LOAD_ROWS)
 CHUNKS = BATCH // CHUNK
 RUN = 4
-VECTOR_COLUMNS = 3 * CHUNK // 16
+MOST_COLUMNS = 3 * CHUNK // 4
 
 FLOPS = 2 * BATCH * FEATURES * DEGREES * OUTPUTS
 
@@ -39,11 +39,11 @@ def words_in_the_same_order(grouped):
     return grouped.rearrange("p (c i) t -> p c t i", i=RUN)
 
 
-def quantise_weights(tc, keep, identity, w):
+def quantise_weights(tc, keep, psum, identity, w):
     nc = tc.nc
     w_codes = keep.tile([P, PASSES, OUTPUTS], U32, align_bytes=64)
     w_scales = keep.tile([P, PASSES, OUTPUTS], U8, align_bytes=64)
-    with tc.tile_pool(name="w_stage", bufs=1) as stage, tc.psum_pool(name="w_psum", bufs=1) as psum:
+    with tc.tile_pool(name="w_stage", bufs=1) as stage:
         w_rows = stage.tile([P, FEATURES * DEGREES], BF16)
         nc.sync.dma_start(out=w_rows[:], in_=w.rearrange("o i n -> o (i n)"))
         by_degree = w_rows[:].rearrange("o (g s q e n) -> o n g q s e", g=4, s=4, q=4, e=2)
@@ -51,7 +51,7 @@ def quantise_weights(tc, keep, identity, w):
         w_grouped = stage.tile([P, PASSES, OUTPUTS, PACK], BF16, align_bytes=64)
         planes_per_bank = 2 * PACK
         for first_pass in range(0, PASSES, 2):
-            w_turned = psum.tile([P, planes_per_bank, OUTPUTS], BF16)
+            w_turned = psum.tile([P, planes_per_bank, OUTPUTS], BF16, tag="sums")
             for k in range(planes_per_bank):
                 degree = WORD_DEGREES[first_pass + k // PACK][k % PACK]
                 plane = w_sorted[:, first_pass * PACK + k, :]
@@ -93,6 +93,8 @@ def tile_function_kernel(tc, x, w, out):
         keep = ctx.enter_context(tc.tile_pool(name="keep", bufs=1))
         identity = keep.tile([P, P], BF16)
         make_identity(nc, identity[:])
+        identity_f32 = keep.tile([P, P], F32)
+        make_identity(nc, identity_f32[:])
         minus_one = keep.tile([P, 1], F32)
         minus_two = keep.tile([P, 1], F32)
         minus_five_halves = keep.tile([P, 1], F32)
@@ -109,7 +111,8 @@ def tile_function_kernel(tc, x, w, out):
         three_rounds = ctx.enter_context(tc.tile_pool(name="three_rounds", bufs=3))
         two_rounds = ctx.enter_context(tc.tile_pool(name="two_rounds", bufs=2))
         five_rounds = ctx.enter_context(tc.tile_pool(name="five_rounds", bufs=5))
-        x_psum = ctx.enter_context(tc.psum_pool(name="x_psum", bufs=5))
+        x_psum = ctx.enter_context(tc.psum_pool(name="x_psum", bufs=4))
+        s3_psum = ctx.enter_context(tc.psum_pool(name="s3_psum", bufs=2))
         out_psum = ctx.enter_context(tc.psum_pool(name="out_psum", bufs=2))
 
         x_loads = x.rearrange("(l p r) f -> l p (r f)", p=P, r=LOAD_ROWS)
@@ -117,7 +120,7 @@ def tile_function_kernel(tc, x, w, out):
 
         x_rows, x_sorted, x_turned = {}, {}, {}
         even_low, odd_low, even_high, odd_high, five = {}, {}, {}, {}, {}
-        grouped, codes, scales, sums = {}, {}, {}, {}
+        s3_copy, grouped, codes, scales, sums = {}, {}, {}, {}, {}
 
         def fetch(load):
             x_rows[load] = loads.tile([P, LOAD_ROWS * FEATURES], BF16, name="x_rows")
@@ -177,35 +180,61 @@ def tile_function_kernel(tc, x, w, out):
             even_high[k] = two_rounds.tile([P, PACK, CHUNK], F32, name="even_high")
             square(even_high[k][:, 0:2, :], odd_low[k][:, 1:3, :], 2.0)
 
+        def copy_s3_to_psum(k):
+            s3_copy[k] = s3_psum.tile([P, CHUNK], F32, name="s3_copy")
+            nc.tensor.matmul(
+                out=s3_copy[k][:], lhsT=identity_f32[:], rhs=even_high[k][:, 0, :], start=True, stop=True
+            )
+
         def s7_and_s6(k):
             square(even_high[k][:, 2, :], odd_low[k][:, 3, :], 2.0)
             square(even_high[k][:, 3, :], even_high[k][:, 0, :], 1.0, minus_two[:])
 
-        def high_odd_products(k):
+        def t9(k):
             odd_high[k] = two_rounds.tile([P, PACK, CHUNK], F32, name="odd_high")
-            s3_twice = even_high[k][:, 0:1, :].to_broadcast([P, 2, CHUNK])
+            shifted_product(odd_high[k][:, 0, :], s3_copy[k][:], 3.0, odd_low[k][:, 1, :])
+
+        def most_of_t11_and_t13(k):
+            s3_twice = s3_copy[k][:].unsqueeze(1).to_broadcast([P, 2, CHUNK])
             shifted_product(odd_high[k][:, 2:4, :], s3_twice, 2.0, odd_low[k][:, 2:4, :])
-            shifted_product(odd_high[k][:, 0:2, :], even_high[k][:, 0:2, :], 3.0, odd_low[k][:, 1:3, :])
 
         def finish_t11_and_t13(k):
             x_twice = x_turned[k][:].unsqueeze(1).to_broadcast([P, 2, CHUNK])
             subtract(odd_high[k][:, 2:4, :], odd_high[k][:, 2:4, :], x_twice)
 
-        def round_odd_low_on_vector(k):
+        def t15(k):
+            shifted_product(odd_high[k][:, 1, :], even_high[k][:, 1, :], 3.0, odd_low[k][:, 2, :])
+
+        def round_most_of_odd_low_on_gpsimd(k):
             grouped[k][ODD_LOW] = three_rounds.tile([P, CHUNK, PACK], BF16, name="odd_low_words", align_bytes=64)
-            nc.vector.tensor_copy(
-                out=words_in_the_same_order(grouped[k][ODD_LOW][:, :VECTOR_COLUMNS, :]),
-                in_=planes_in_word_order(odd_low[k][:, :, :VECTOR_COLUMNS]),
+            nc.gpsimd.tensor_scalar(
+                out=words_in_the_same_order(grouped[k][ODD_LOW][:, :MOST_COLUMNS, :]),
+                in0=planes_in_word_order(odd_low[k][:, :, :MOST_COLUMNS]),
+                scalar1=1.0,
+                scalar2=0.0,
+                op0=ALU.mult,
+                op1=ALU.add,
             )
 
-        def round_odd_high(k):
-            grouped[k][ODD_HIGH] = two_rounds.tile([P, CHUNK, PACK], BF16, name="odd_high_words", align_bytes=64)
+        def round_the_rest_of_the_odd_words(low, high):
+            if is_chunk(high):
+                grouped[high][ODD_HIGH] = two_rounds.tile(
+                    [P, CHUNK, PACK], BF16, name="odd_high_words", align_bytes=64
+                )
+            for k, c, values in ((low, ODD_LOW, odd_low), (high, ODD_HIGH, odd_high)):
+                if is_chunk(k):
+                    nc.scalar.copy(
+                        out=words_in_the_same_order(grouped[k][c][:, MOST_COLUMNS:, :]),
+                        in_=planes_in_word_order(values[k][:, :, MOST_COLUMNS:]),
+                    )
+
+        def round_most_of_odd_high(k):
             nc.vector.tensor_copy(
-                out=words_in_the_same_order(grouped[k][ODD_HIGH][:]),
-                in_=planes_in_word_order(odd_high[k][:]),
+                out=words_in_the_same_order(grouped[k][ODD_HIGH][:, :MOST_COLUMNS, :]),
+                in_=planes_in_word_order(odd_high[k][:, :, :MOST_COLUMNS]),
             )
 
-        def round_on_scalar(k):
+        def round_even_high(k):
             grouped[k][EVEN_HIGH] = three_rounds.tile([P, CHUNK, PACK], BF16, name="even_high_words", align_bytes=64)
             nc.scalar.activation(
                 out=words_in_the_same_order(grouped[k][EVEN_HIGH][:]),
@@ -213,10 +242,6 @@ def tile_function_kernel(tc, x, w, out):
                 func=ACT.Identity,
                 scale=0.5,
                 bias=minus_one[:],
-            )
-            nc.scalar.copy(
-                out=words_in_the_same_order(grouped[k][ODD_LOW][:, VECTOR_COLUMNS:, :]),
-                in_=planes_in_word_order(odd_low[k][:, :, VECTOR_COLUMNS:]),
             )
 
         def quantise(k):
@@ -260,19 +285,25 @@ def tile_function_kernel(tc, x, w, out):
             fetch(1)
             sort_features(0)
             turn(0)
-            w_codes, w_scales = quantise_weights(tc, keep, identity[:], w)
+            w_codes, w_scales = quantise_weights(tc, keep, out_psum, identity[:], w)
             for j in range(-2, CHUNKS + 3):
-                if is_chunk(j + 2):
-                    squares_from_x(j + 2)
-                    round_even_low_on_gpsimd(j + 2)
+                if is_chunk(j):
+                    finish_t7(j)
+                    round_most_of_odd_low_on_gpsimd(j)
+                    s7_and_s6(j)
                 if is_chunk(j - 1):
                     finish_t11_and_t13(j - 1)
                 if is_chunk(j):
-                    finish_t7(j)
-                    s7_and_s6(j)
+                    t9(j)
+                round_the_rest_of_the_odd_words(j, j - 1)
+                if is_chunk(j + 2):
+                    squares_from_x(j + 2)
+                    round_even_low_on_gpsimd(j + 2)
                 if is_chunk(j + 1):
                     t5_and_t3(j + 1)
                     s3_and_s5(j + 1)
+                if is_chunk(j):
+                    most_of_t11_and_t13(j)
                 if is_chunk(j + 3):
                     if (j + 3) % CHUNKS_PER_LOAD == 0:
                         load = (j + 3) // CHUNKS_PER_LOAD
@@ -280,17 +311,17 @@ def tile_function_kernel(tc, x, w, out):
                             fetch(load + 1)
                         sort_features(load)
                     turn(j + 3)
-                if is_chunk(j):
-                    round_odd_low_on_vector(j)
-                    round_on_scalar(j)
+                if is_chunk(j + 1):
+                    copy_s3_to_psum(j + 1)
+                if is_chunk(j - 1):
+                    round_most_of_odd_high(j - 1)
                 if is_chunk(j + 1):
                     most_of_t7(j + 1)
-                if is_chunk(j - 1):
-                    round_odd_high(j - 1)
+                if is_chunk(j):
+                    t15(j)
+                    round_even_high(j)
                 if is_chunk(j - 2):
                     quantise(j - 2)
                     multiply(j - 2)
-                if is_chunk(j):
-                    high_odd_products(j)
                 if is_chunk(j - 3):
                     store(j - 3)

@@ -20,13 +20,18 @@ WORD_DEGREES = ((0, 2, 4, 8), (1, 3, 5, 7), (6, 10, 14, 12), (9, 15, 11, 13))
 EVEN_LOW, ODD_LOW, EVEN_HIGH, ODD_HIGH = 0, 1, 2, 3
 
 CHUNK = 512
-TILES = CHUNK // P
 LOAD_ROWS = 16
-CHUNKS_PER_LOAD = LOAD_ROWS // TILES
 LOADS = BATCH // (P * LOAD_ROWS)
-CHUNKS = BATCH // CHUNK
+RAMP_UP, RAMP_DOWN = (1, 1, 2), (2, 1, 1)
+FULL = CHUNK // P
+CHUNK_TILES = RAMP_UP + (FULL,) * ((BATCH // P - sum(RAMP_UP + RAMP_DOWN)) // FULL) + RAMP_DOWN
+CHUNKS = len(CHUNK_TILES)
+FIRST_TILE = tuple(sum(CHUNK_TILES[:k]) for k in range(CHUNKS))
+PIECES = ((0, slice(0, FULL)), (0, slice(FULL, LOAD_ROWS))) + tuple(
+    (load, slice(0, LOAD_ROWS)) for load in range(1, LOADS)
+)
+PIECE_AT = {load * LOAD_ROWS + rows.start: piece for piece, (load, rows) in enumerate(PIECES)}
 RUN = 4
-MOST_COLUMNS = 3 * CHUNK // 4
 
 FLOPS = 2 * BATCH * FEATURES * DEGREES * OUTPUTS
 
@@ -37,39 +42,6 @@ def planes_in_word_order(planes):
 
 def words_in_the_same_order(grouped):
     return grouped.rearrange("p (c i) t -> p c t i", i=RUN)
-
-
-def quantise_weights(tc, keep, psum, identity, w):
-    nc = tc.nc
-    w_codes = keep.tile([P, PASSES, OUTPUTS], U32, align_bytes=64)
-    w_scales = keep.tile([P, PASSES, OUTPUTS], U8, align_bytes=64)
-    with tc.tile_pool(name="w_stage", bufs=1) as stage:
-        w_rows = stage.tile([P, FEATURES * DEGREES], BF16)
-        nc.sync.dma_start(out=w_rows[:], in_=w.rearrange("o i n -> o (i n)"))
-        by_degree = w_rows[:].rearrange("o (g s q e n) -> o n g q s e", g=4, s=4, q=4, e=2)
-        w_sorted = stage.tile([P, DEGREES, FEATURES], BF16)
-        w_grouped = stage.tile([P, PASSES, OUTPUTS, PACK], BF16, align_bytes=64)
-        planes_per_bank = 2 * PACK
-        for first_pass in range(0, PASSES, 2):
-            w_turned = psum.tile([P, planes_per_bank, OUTPUTS], BF16, tag="sums")
-            for k in range(planes_per_bank):
-                degree = WORD_DEGREES[first_pass + k // PACK][k % PACK]
-                plane = w_sorted[:, first_pass * PACK + k, :]
-                nc.vector.tensor_copy(
-                    out=plane.rearrange("o (g q s e) -> o g q s e", g=4, q=4, s=4),
-                    in_=by_degree[:, degree],
-                )
-                nc.tensor.transpose(w_turned[:, k, :], plane, identity)
-            nc.vector.tensor_copy(
-                out=w_grouped[:, first_pass : first_pass + 2, :, :],
-                in_=w_turned[:].rearrange("p (c t) o -> p c o t", t=PACK),
-            )
-        nc.vector.quantize_mx(
-            out=w_codes[:].rearrange("p c o -> p (c o)").bitcast(FP8X4),
-            scales=w_scales[:].rearrange("p c o -> p (c o)"),
-            in_=w_grouped[:].rearrange("p c o t -> p (c o t)"),
-        )
-    return w_codes, w_scales
 
 
 def tile_function_kernel(tc, x, w, out):
@@ -107,7 +79,8 @@ def tile_function_kernel(tc, x, w, out):
             nc.gpsimd.memset(fixed[:, 0, :], 4.0)
             even_low_planes.append(fixed)
 
-        loads = ctx.enter_context(tc.tile_pool(name="loads", bufs=2))
+        stage = ctx.enter_context(tc.tile_pool(name="w_stage", bufs=1))
+        loads = ctx.enter_context(tc.tile_pool(name="loads", bufs=3))
         three_rounds = ctx.enter_context(tc.tile_pool(name="three_rounds", bufs=3))
         two_rounds = ctx.enter_context(tc.tile_pool(name="two_rounds", bufs=2))
         five_rounds = ctx.enter_context(tc.tile_pool(name="five_rounds", bufs=5))
@@ -122,44 +95,86 @@ def tile_function_kernel(tc, x, w, out):
         even_low, odd_low, even_high, odd_high, five = {}, {}, {}, {}, {}
         s3_copy, grouped, codes, scales, sums = {}, {}, {}, {}, {}
 
-        def fetch(load):
-            x_rows[load] = loads.tile([P, LOAD_ROWS * FEATURES], BF16, name="x_rows")
-            nc.sync.dma_start(out=x_rows[load][:], in_=x_loads[load])
+        w_codes = keep.tile([P, PASSES, OUTPUTS], U32, align_bytes=64)
+        w_scales = keep.tile([P, PASSES, OUTPUTS], U8, align_bytes=64)
+        w_rows = stage.tile([P, FEATURES * DEGREES], BF16)
+        w_sorted = stage.tile([P, DEGREES, FEATURES], BF16)
+        w_grouped = stage.tile([P, PASSES, OUTPUTS, PACK], BF16, align_bytes=64)
 
-        def sort_features(load):
-            x_sorted[load] = loads.tile([P, LOAD_ROWS * FEATURES], BF16, name="x_sorted")
+        def fetch_weights():
+            nc.sync.dma_start(out=w_rows[:], in_=w.rearrange("o i n -> o (i n)"))
+
+        def turn_weights(first_pass):
+            by_degree = w_rows[:].rearrange("o (g s q e n) -> o n g q s e", g=4, s=4, q=4, e=2)
+            w_turned = out_psum.tile([P, 2 * PACK, OUTPUTS], BF16, tag="sums")
+            for k in range(2 * PACK):
+                degree = WORD_DEGREES[first_pass + k // PACK][k % PACK]
+                plane = w_sorted[:, first_pass * PACK + k, :]
+                nc.vector.tensor_copy(
+                    out=plane.rearrange("o (g q s e) -> o g q s e", g=4, q=4, s=4),
+                    in_=by_degree[:, degree],
+                )
+                nc.tensor.transpose(w_turned[:, k, :], plane, identity[:])
             nc.vector.tensor_copy(
-                out=x_sorted[load][:].bitcast(F32).rearrange("p (a q s) -> p a q s", q=4, s=4),
-                in_=x_rows[load][:].bitcast(F32).rearrange("p (a s q) -> p a q s", q=4, s=4),
+                out=w_grouped[:, first_pass : first_pass + 2, :, :],
+                in_=w_turned[:].rearrange("p (c t) o -> p c o t", t=PACK),
+            )
+
+        def quantise_weights():
+            nc.vector.quantize_mx(
+                out=w_codes[:].rearrange("p c o -> p (c o)").bitcast(FP8X4),
+                scales=w_scales[:].rearrange("p c o -> p (c o)"),
+                in_=w_grouped[:].rearrange("p c o t -> p (c o t)"),
+            )
+
+        def columns(k):
+            return slice(0, CHUNK_TILES[k] * P)
+
+        def fetch(piece):
+            load, rows = PIECES[piece]
+            if rows.start == 0:
+                x_rows[load] = loads.tile([P, LOAD_ROWS * FEATURES], BF16, name="x_rows")
+                x_sorted[load] = loads.tile([P, LOAD_ROWS * FEATURES], BF16, name="x_sorted")
+            part = slice(rows.start * FEATURES, rows.stop * FEATURES)
+            nc.sync.dma_start(out=x_rows[load][:, part], in_=x_loads[load][:, part])
+
+        def sort_features(piece):
+            load, rows = PIECES[piece]
+            part = slice(rows.start * FEATURES, rows.stop * FEATURES)
+            nc.vector.tensor_copy(
+                out=x_sorted[load][:, part].bitcast(F32).rearrange("p (a q s) -> p a q s", q=4, s=4),
+                in_=x_rows[load][:, part].bitcast(F32).rearrange("p (a s q) -> p a q s", q=4, s=4),
             )
 
         def turn(k):
-            x_turned[k] = x_psum.tile([P, CHUNK], BF16, name="x_turned")
-            for r in range(TILES):
-                row = (k % CHUNKS_PER_LOAD) * TILES + r
+            x_turned[k] = x_psum.tile([P, CHUNK], BF16, name="x_turned")[:, columns(k)]
+            for r in range(CHUNK_TILES[k]):
+                load, row = divmod(FIRST_TILE[k] + r, LOAD_ROWS)
                 nc.tensor.transpose(
                     x_turned[k][:, r * P : (r + 1) * P],
-                    x_sorted[k // CHUNKS_PER_LOAD][:, row * FEATURES : (row + 1) * FEATURES],
+                    x_sorted[load][:, row * FEATURES : (row + 1) * FEATURES],
                     identity[:],
                 )
 
         def squares_from_x(k):
-            even_low[k] = even_low_planes[k % 2]
-            odd_low[k] = three_rounds.tile([P, PACK, CHUNK], F32, name="odd_low")
-            five[k] = two_rounds.tile([P, CHUNK], F32, name="five")
+            even_low[k] = even_low_planes[k % 2][:, :, columns(k)]
+            odd_low[k] = three_rounds.tile([P, PACK, CHUNK], F32, name="odd_low")[:, :, columns(k)]
+            five[k] = two_rounds.tile([P, CHUNK], F32, name="five")[:, columns(k)]
             s1, s2, s4 = (even_low[k][:, t, :] for t in range(1, PACK))
-            square(s1, x_turned[k][:], 2.0)
-            nc.scalar.copy(out=odd_low[k][:, 0, :], in_=x_turned[k][:])
+            square(s1, x_turned[k], 2.0)
+            nc.scalar.copy(out=odd_low[k][:, 0, :], in_=x_turned[k])
             square(s2, s1, 1.0, minus_two[:])
-            square(five[k][:], s1, 1.0, minus_five_halves[:])
+            square(five[k], s1, 1.0, minus_five_halves[:])
             square(s4, s2, 1.0, minus_two[:])
 
         def round_even_low_on_gpsimd(k):
             grouped[k] = {}
-            grouped[k][EVEN_LOW] = five_rounds.tile([P, CHUNK, PACK], BF16, name="even_low_words", align_bytes=64)
+            grouped[k][EVEN_LOW] = five_rounds.tile(
+                [P, CHUNK, PACK], BF16, name="even_low_words", align_bytes=64
+            )[:, columns(k), :]
             nc.gpsimd.tensor_scalar(
-                out=words_in_the_same_order(grouped[k][EVEN_LOW][:]),
-                in0=planes_in_word_order(even_low[k][:]),
+                out=words_in_the_same_order(grouped[k][EVEN_LOW]),
+                in0=planes_in_word_order(even_low[k]),
                 scalar1=0.5,
                 scalar2=-1.0,
                 op0=ALU.mult,
@@ -167,23 +182,23 @@ def tile_function_kernel(tc, x, w, out):
             )
 
         def t5_and_t3(k):
-            shifted_product(odd_low[k][:, 2, :], five[k][:], 1.25, x_turned[k][:])
-            shifted_product(odd_low[k][:, 1, :], even_low[k][:, 1, :], 3.0, x_turned[k][:])
+            shifted_product(odd_low[k][:, 2, :], five[k], 1.25, x_turned[k])
+            shifted_product(odd_low[k][:, 1, :], even_low[k][:, 1, :], 3.0, x_turned[k])
 
         def most_of_t7(k):
             shifted_product(odd_low[k][:, 3, :], even_low[k][:, 2, :], 2.0, odd_low[k][:, 1, :])
 
         def finish_t7(k):
-            subtract(odd_low[k][:, 3, :], odd_low[k][:, 3, :], x_turned[k][:])
+            subtract(odd_low[k][:, 3, :], odd_low[k][:, 3, :], x_turned[k])
 
         def s3_and_s5(k):
-            even_high[k] = two_rounds.tile([P, PACK, CHUNK], F32, name="even_high")
+            even_high[k] = two_rounds.tile([P, PACK, CHUNK], F32, name="even_high")[:, :, columns(k)]
             square(even_high[k][:, 0:2, :], odd_low[k][:, 1:3, :], 2.0)
 
         def copy_s3_to_psum(k):
-            s3_copy[k] = s3_psum.tile([P, CHUNK], F32, name="s3_copy")
+            s3_copy[k] = s3_psum.tile([P, CHUNK], F32, name="s3_copy")[:, columns(k)]
             nc.tensor.matmul(
-                out=s3_copy[k][:], lhsT=identity_f32[:], rhs=even_high[k][:, 0, :], start=True, stop=True
+                out=s3_copy[k], lhsT=identity_f32[:], rhs=even_high[k][:, 0, :], start=True, stop=True
             )
 
         def s7_and_s6(k):
@@ -191,25 +206,31 @@ def tile_function_kernel(tc, x, w, out):
             square(even_high[k][:, 3, :], even_high[k][:, 0, :], 1.0, minus_two[:])
 
         def t9(k):
-            odd_high[k] = two_rounds.tile([P, PACK, CHUNK], F32, name="odd_high")
-            shifted_product(odd_high[k][:, 0, :], s3_copy[k][:], 3.0, odd_low[k][:, 1, :])
+            odd_high[k] = two_rounds.tile([P, PACK, CHUNK], F32, name="odd_high")[:, :, columns(k)]
+            shifted_product(odd_high[k][:, 0, :], s3_copy[k], 3.0, odd_low[k][:, 1, :])
+
+        def twice(plane, k):
+            return plane.unsqueeze(1).to_broadcast([P, 2, CHUNK_TILES[k] * P])
 
         def most_of_t11_and_t13(k):
-            s3_twice = s3_copy[k][:].unsqueeze(1).to_broadcast([P, 2, CHUNK])
-            shifted_product(odd_high[k][:, 2:4, :], s3_twice, 2.0, odd_low[k][:, 2:4, :])
+            shifted_product(odd_high[k][:, 2:4, :], twice(s3_copy[k], k), 2.0, odd_low[k][:, 2:4, :])
 
         def finish_t11_and_t13(k):
-            x_twice = x_turned[k][:].unsqueeze(1).to_broadcast([P, 2, CHUNK])
-            subtract(odd_high[k][:, 2:4, :], odd_high[k][:, 2:4, :], x_twice)
+            subtract(odd_high[k][:, 2:4, :], odd_high[k][:, 2:4, :], twice(x_turned[k], k))
 
         def t15(k):
             shifted_product(odd_high[k][:, 1, :], even_high[k][:, 1, :], 3.0, odd_low[k][:, 2, :])
 
+        def most_columns(k):
+            return CHUNK_TILES[k] * P * 3 // 4
+
         def round_most_of_odd_low_on_gpsimd(k):
-            grouped[k][ODD_LOW] = three_rounds.tile([P, CHUNK, PACK], BF16, name="odd_low_words", align_bytes=64)
+            grouped[k][ODD_LOW] = three_rounds.tile(
+                [P, CHUNK, PACK], BF16, name="odd_low_words", align_bytes=64
+            )[:, columns(k), :]
             nc.gpsimd.tensor_scalar(
-                out=words_in_the_same_order(grouped[k][ODD_LOW][:, :MOST_COLUMNS, :]),
-                in0=planes_in_word_order(odd_low[k][:, :, :MOST_COLUMNS]),
+                out=words_in_the_same_order(grouped[k][ODD_LOW][:, : most_columns(k), :]),
+                in0=planes_in_word_order(odd_low[k][:, :, : most_columns(k)]),
                 scalar1=1.0,
                 scalar2=0.0,
                 op0=ALU.mult,
@@ -220,25 +241,27 @@ def tile_function_kernel(tc, x, w, out):
             if is_chunk(high):
                 grouped[high][ODD_HIGH] = two_rounds.tile(
                     [P, CHUNK, PACK], BF16, name="odd_high_words", align_bytes=64
-                )
+                )[:, columns(high), :]
             for k, c, values in ((low, ODD_LOW, odd_low), (high, ODD_HIGH, odd_high)):
                 if is_chunk(k):
                     nc.scalar.copy(
-                        out=words_in_the_same_order(grouped[k][c][:, MOST_COLUMNS:, :]),
-                        in_=planes_in_word_order(values[k][:, :, MOST_COLUMNS:]),
+                        out=words_in_the_same_order(grouped[k][c][:, most_columns(k) :, :]),
+                        in_=planes_in_word_order(values[k][:, :, most_columns(k) :]),
                     )
 
         def round_most_of_odd_high(k):
             nc.vector.tensor_copy(
-                out=words_in_the_same_order(grouped[k][ODD_HIGH][:, :MOST_COLUMNS, :]),
-                in_=planes_in_word_order(odd_high[k][:, :, :MOST_COLUMNS]),
+                out=words_in_the_same_order(grouped[k][ODD_HIGH][:, : most_columns(k), :]),
+                in_=planes_in_word_order(odd_high[k][:, :, : most_columns(k)]),
             )
 
         def round_even_high(k):
-            grouped[k][EVEN_HIGH] = three_rounds.tile([P, CHUNK, PACK], BF16, name="even_high_words", align_bytes=64)
+            grouped[k][EVEN_HIGH] = three_rounds.tile(
+                [P, CHUNK, PACK], BF16, name="even_high_words", align_bytes=64
+            )[:, columns(k), :]
             nc.scalar.activation(
-                out=words_in_the_same_order(grouped[k][EVEN_HIGH][:]),
-                in_=planes_in_word_order(even_high[k][:]),
+                out=words_in_the_same_order(grouped[k][EVEN_HIGH]),
+                in_=planes_in_word_order(even_high[k]),
                 func=ACT.Identity,
                 scale=0.5,
                 bias=minus_one[:],
@@ -249,20 +272,20 @@ def tile_function_kernel(tc, x, w, out):
             scales[k] = two_rounds.tile([P, PASSES, CHUNK], U8, name="scales", align_bytes=64)
             for c in range(PASSES):
                 nc.vector.quantize_mx(
-                    out=codes[k][:, c, :].bitcast(FP8X4),
-                    scales=scales[k][:, c, :],
-                    in_=grouped[k][c][:].rearrange("p w t -> p (w t)"),
+                    out=codes[k][:, c, columns(k)].bitcast(FP8X4),
+                    scales=scales[k][:, c, columns(k)],
+                    in_=grouped[k][c].rearrange("p w t -> p (w t)"),
                 )
 
         def multiply(k):
-            sums[k] = out_psum.tile([P, TILES, OUTPUTS], F32, name="sums")
-            for r in range(TILES):
-                columns = slice(r * P, (r + 1) * P)
+            sums[k] = out_psum.tile([P, FULL, OUTPUTS], F32, name="sums")[:, : CHUNK_TILES[k], :]
+            for r in range(CHUNK_TILES[k]):
+                tile_columns = slice(r * P, (r + 1) * P)
                 for c in range(PASSES):
                     nc.tensor.matmul_mx(
                         out=sums[k][:, r, :],
-                        lhsT=codes[k][:, c, columns].bitcast(FP8X4),
-                        lhsT_scale=scales[k][:, c, columns],
+                        lhsT=codes[k][:, c, tile_columns].bitcast(FP8X4),
+                        lhsT_scale=scales[k][:, c, tile_columns],
                         rhs=w_codes[:, c, :].bitcast(FP8X4),
                         rhs_scale=w_scales[:, c, :],
                         start=(c == 0),
@@ -270,23 +293,19 @@ def tile_function_kernel(tc, x, w, out):
                     )
 
         def store(k):
-            result = three_rounds.tile([P, TILES, OUTPUTS], F32, name="result")
-            nc.scalar.copy(out=result[:], in_=sums[k][:])
-            first_row = (k % CHUNKS_PER_LOAD) * TILES
-            nc.sync.dma_start(
-                out=out_loads[k // CHUNKS_PER_LOAD][:, first_row : first_row + TILES, :], in_=result[:]
-            )
+            result = three_rounds.tile([P, FULL, OUTPUTS], F32, name="result")[:, : CHUNK_TILES[k], :]
+            nc.scalar.copy(out=result, in_=sums[k])
+            load, row = divmod(FIRST_TILE[k], LOAD_ROWS)
+            nc.sync.dma_start(out=out_loads[load][:, row : row + CHUNK_TILES[k], :], in_=result)
 
         def is_chunk(k):
             return 0 <= k < CHUNKS
 
         fetch(0)
+        fetch_weights()
+        fetch(1)
         with tc.manual_schedule():
-            fetch(1)
-            sort_features(0)
-            turn(0)
-            w_codes, w_scales = quantise_weights(tc, keep, out_psum, identity[:], w)
-            for j in range(-2, CHUNKS + 3):
+            for j in range(-3, CHUNKS + 3):
                 if is_chunk(j):
                     finish_t7(j)
                     round_most_of_odd_low_on_gpsimd(j)
@@ -305,11 +324,11 @@ def tile_function_kernel(tc, x, w, out):
                 if is_chunk(j):
                     most_of_t11_and_t13(j)
                 if is_chunk(j + 3):
-                    if (j + 3) % CHUNKS_PER_LOAD == 0:
-                        load = (j + 3) // CHUNKS_PER_LOAD
-                        if load + 1 < LOADS:
-                            fetch(load + 1)
-                        sort_features(load)
+                    if FIRST_TILE[j + 3] in PIECE_AT:
+                        piece = PIECE_AT[FIRST_TILE[j + 3]]
+                        if piece + 2 < len(PIECES):
+                            fetch(piece + 2)
+                        sort_features(piece)
                     turn(j + 3)
                 if is_chunk(j + 1):
                     copy_s3_to_psum(j + 1)
@@ -320,6 +339,12 @@ def tile_function_kernel(tc, x, w, out):
                 if is_chunk(j):
                     t15(j)
                     round_even_high(j)
+                if j == -2:
+                    turn_weights(0)
+                if j == -1:
+                    turn_weights(2)
+                if j == 0:
+                    quantise_weights()
                 if is_chunk(j - 2):
                     quantise(j - 2)
                     multiply(j - 2)

@@ -74,7 +74,7 @@ def tile_function_kernel(tc, x, w, out):
         nc.vector.memset(minus_two[:], -2.0)
         nc.vector.memset(minus_five_halves[:], -2.5)
         even_low_planes = []
-        for k in range(2):
+        for k in range(3):
             fixed = keep.tile([P, PACK, CHUNK], F32, name="even_low_planes_%d" % k)
             nc.gpsimd.memset(fixed[:, 0, :], 4.0)
             even_low_planes.append(fixed)
@@ -157,7 +157,7 @@ def tile_function_kernel(tc, x, w, out):
                 )
 
         def squares_from_x(k):
-            even_low[k] = even_low_planes[k % 2][:, :, columns(k)]
+            even_low[k] = even_low_planes[k % 3][:, :, columns(k)]
             odd_low[k] = three_rounds.tile([P, PACK, CHUNK], F32, name="odd_low")[:, :, columns(k)]
             five[k] = two_rounds.tile([P, CHUNK], F32, name="five")[:, columns(k)]
             s1, s2, s4 = (even_low[k][:, t, :] for t in range(1, PACK))
@@ -205,54 +205,56 @@ def tile_function_kernel(tc, x, w, out):
             square(even_high[k][:, 2, :], odd_low[k][:, 3, :], 2.0)
             square(even_high[k][:, 3, :], even_high[k][:, 0, :], 1.0, minus_two[:])
 
-        def t9(k):
-            odd_high[k] = two_rounds.tile([P, PACK, CHUNK], F32, name="odd_high")[:, :, columns(k)]
-            shifted_product(odd_high[k][:, 0, :], s3_copy[k], 3.0, odd_low[k][:, 1, :])
+        def fused(k):
+            return CHUNK_TILES[k] * P * 5 // 8
 
-        def twice(plane, k):
-            return plane.unsqueeze(1).to_broadcast([P, 2, CHUNK_TILES[k] * P])
+        def twice(plane):
+            return plane.unsqueeze(1).to_broadcast([P, 2, plane.shape[-1]])
 
         def most_of_t11_and_t13(k):
-            shifted_product(odd_high[k][:, 2:4, :], twice(s3_copy[k], k), 2.0, odd_low[k][:, 2:4, :])
+            odd_high[k] = two_rounds.tile([P, PACK, CHUNK], F32, name="odd_high")[:, :, columns(k)]
+            shifted_product(odd_high[k][:, 2:4, :], twice(s3_copy[k]), 2.0, odd_low[k][:, 2:4, :])
 
-        def finish_t11_and_t13(k):
-            subtract(odd_high[k][:, 2:4, :], odd_high[k][:, 2:4, :], twice(x_turned[k], k))
+        def most_of_t9_and_t15(k):
+            f = fused(k)
+            shifted_product(
+                odd_high[k][:, 0:2, :f], even_low[k][:, 2:4, :f], 2.0, odd_low[k][:, 2:4, :f]
+            )
+            shifted_product(
+                odd_high[k][:, 0:2, f:], even_high[k][:, 0:2, f:], 3.0, odd_low[k][:, 1:3, f:]
+            )
 
-        def t15(k):
-            shifted_product(odd_high[k][:, 1, :], even_high[k][:, 1, :], 3.0, odd_low[k][:, 2, :])
+        def finish_and_round_odd_high(k):
+            f = fused(k)
+            grouped[k][ODD_HIGH] = two_rounds.tile(
+                [P, CHUNK, PACK], BF16, name="odd_high_words", align_bytes=64
+            )[:, columns(k), :]
+            x_run = x_turned[k][:, :f].rearrange("p (c i) -> p c i", i=RUN).unsqueeze(2)
+            subtract(
+                words_in_the_same_order(grouped[k][ODD_HIGH][:, :f, :]),
+                planes_in_word_order(odd_high[k][:, :, :f]),
+                x_run.to_broadcast([P, f // RUN, PACK, RUN]),
+            )
+            subtract(odd_high[k][:, 2:4, f:], odd_high[k][:, 2:4, f:], twice(x_turned[k][:, f:]))
 
-        def most_columns(k):
-            return CHUNK_TILES[k] * P * 3 // 4
+        def round_the_rest_of_odd_high(k):
+            f = fused(k)
+            nc.scalar.copy(
+                out=words_in_the_same_order(grouped[k][ODD_HIGH][:, f:, :]),
+                in_=planes_in_word_order(odd_high[k][:, :, f:]),
+            )
 
-        def round_most_of_odd_low_on_gpsimd(k):
+        def round_odd_low_on_gpsimd(k):
             grouped[k][ODD_LOW] = three_rounds.tile(
                 [P, CHUNK, PACK], BF16, name="odd_low_words", align_bytes=64
             )[:, columns(k), :]
             nc.gpsimd.tensor_scalar(
-                out=words_in_the_same_order(grouped[k][ODD_LOW][:, : most_columns(k), :]),
-                in0=planes_in_word_order(odd_low[k][:, :, : most_columns(k)]),
+                out=words_in_the_same_order(grouped[k][ODD_LOW]),
+                in0=planes_in_word_order(odd_low[k]),
                 scalar1=1.0,
                 scalar2=0.0,
                 op0=ALU.mult,
                 op1=ALU.add,
-            )
-
-        def round_the_rest_of_the_odd_words(low, high):
-            if is_chunk(high):
-                grouped[high][ODD_HIGH] = two_rounds.tile(
-                    [P, CHUNK, PACK], BF16, name="odd_high_words", align_bytes=64
-                )[:, columns(high), :]
-            for k, c, values in ((low, ODD_LOW, odd_low), (high, ODD_HIGH, odd_high)):
-                if is_chunk(k):
-                    nc.scalar.copy(
-                        out=words_in_the_same_order(grouped[k][c][:, most_columns(k) :, :]),
-                        in_=planes_in_word_order(values[k][:, :, most_columns(k) :]),
-                    )
-
-        def round_most_of_odd_high(k):
-            nc.vector.tensor_copy(
-                out=words_in_the_same_order(grouped[k][ODD_HIGH][:, : most_columns(k), :]),
-                in_=planes_in_word_order(odd_high[k][:, :, : most_columns(k)]),
             )
 
         def round_even_high(k):
@@ -308,13 +310,11 @@ def tile_function_kernel(tc, x, w, out):
             for j in range(-3, CHUNKS + 3):
                 if is_chunk(j):
                     finish_t7(j)
-                    round_most_of_odd_low_on_gpsimd(j)
+                    round_odd_low_on_gpsimd(j)
                     s7_and_s6(j)
                 if is_chunk(j - 1):
-                    finish_t11_and_t13(j - 1)
-                if is_chunk(j):
-                    t9(j)
-                round_the_rest_of_the_odd_words(j, j - 1)
+                    finish_and_round_odd_high(j - 1)
+                    round_the_rest_of_odd_high(j - 1)
                 if is_chunk(j + 2):
                     squares_from_x(j + 2)
                     round_even_low_on_gpsimd(j + 2)
@@ -332,12 +332,11 @@ def tile_function_kernel(tc, x, w, out):
                     turn(j + 3)
                 if is_chunk(j + 1):
                     copy_s3_to_psum(j + 1)
-                if is_chunk(j - 1):
-                    round_most_of_odd_high(j - 1)
+                if is_chunk(j):
+                    most_of_t9_and_t15(j)
                 if is_chunk(j + 1):
                     most_of_t7(j + 1)
                 if is_chunk(j):
-                    t15(j)
                     round_even_high(j)
                 if j == -2:
                     turn_weights(0)

@@ -33,6 +33,8 @@ PIECES = ((0, slice(0, FULL)), (0, slice(FULL, LOAD_ROWS))) + tuple(
 PIECE_AT = {load * LOAD_ROWS + rows.start: piece for piece, (load, rows) in enumerate(PIECES)}
 RUN = 4
 
+FUSED, GIVEN = 18, 4
+
 FLOPS = 2 * BATCH * FEATURES * DEGREES * OUTPUTS
 
 
@@ -85,37 +87,35 @@ def tile_function_kernel(tc, x, w, out):
         two_rounds = ctx.enter_context(tc.tile_pool(name="two_rounds", bufs=2))
         five_rounds = ctx.enter_context(tc.tile_pool(name="five_rounds", bufs=5))
         x_psum = ctx.enter_context(tc.psum_pool(name="x_psum", bufs=4))
-        s3_psum = ctx.enter_context(tc.psum_pool(name="s3_psum", bufs=2))
-        out_psum = ctx.enter_context(tc.psum_pool(name="out_psum", bufs=2))
+        s2_psum = ctx.enter_context(tc.psum_pool(name="s2_psum", bufs=2))
+        s3_psum = ctx.enter_context(tc.psum_pool(name="s3_psum", bufs=1))
+        out_psum = ctx.enter_context(tc.psum_pool(name="out_psum", bufs=1))
 
         x_loads = x.rearrange("(l p r) f -> l p (r f)", p=P, r=LOAD_ROWS)
         out_loads = out.rearrange("(l p r) o -> l p r o", p=P, r=LOAD_ROWS)
 
         x_rows, x_sorted, x_turned = {}, {}, {}
         even_low, odd_low, even_high, odd_high, five = {}, {}, {}, {}, {}
-        s3_copy, grouped, codes, scales, sums = {}, {}, {}, {}, {}
+        s2_copy, s3_copy, grouped, high_words, codes, scales, sums = {}, {}, {}, {}, {}, {}, {}
 
         w_codes = keep.tile([P, PASSES, OUTPUTS], U32, align_bytes=64)
         w_scales = keep.tile([P, PASSES, OUTPUTS], U8, align_bytes=64)
         w_rows = stage.tile([P, FEATURES * DEGREES], BF16)
-        w_sorted = stage.tile([P, DEGREES, FEATURES], BF16)
         w_grouped = stage.tile([P, PASSES, OUTPUTS, PACK], BF16, align_bytes=64)
 
         def fetch_weights():
-            nc.sync.dma_start(out=w_rows[:], in_=w.rearrange("o i n -> o (i n)"))
+            w_pairs = w.rearrange("o (g s q e) n -> o g q s (e n)", g=4, s=4, q=4, e=2)
+            sorted_pairs = w_rows[:].rearrange("o (g q s m) -> o g q s m", g=4, q=4, s=4)
+            for g in range(4):
+                for q in range(4):
+                    nc.sync.dma_start(out=sorted_pairs[:, g, q], in_=w_pairs[:, g, q])
 
         def turn_weights(first_pass):
-            by_degree = w_rows[:].rearrange("o (g s q e n) -> o n g q s e", g=4, s=4, q=4, e=2)
             w_turned = out_psum.tile([P, 2 * PACK, OUTPUTS], BF16, tag="sums")
             for k in range(2 * PACK):
                 degree = WORD_DEGREES[first_pass + k // PACK][k % PACK]
-                plane = w_sorted[:, first_pass * PACK + k, :]
-                nc.vector.tensor_copy(
-                    out=plane.rearrange("o (g q s e) -> o g q s e", g=4, q=4, s=4),
-                    in_=by_degree[:, degree],
-                )
-                nc.tensor.transpose(w_turned[:, k, :], plane, identity[:])
-            nc.vector.tensor_copy(
+                nc.tensor.transpose(w_turned[:, k, :], w_rows[:, degree : FEATURES * DEGREES : DEGREES], identity[:])
+            nc.scalar.copy(
                 out=w_grouped[:, first_pass : first_pass + 2, :, :],
                 in_=w_turned[:].rearrange("p (c t) o -> p c o t", t=PACK),
             )
@@ -168,12 +168,10 @@ def tile_function_kernel(tc, x, w, out):
             square(s4, s2, 1.0, minus_two[:])
 
         def round_even_low_on_gpsimd(k):
-            grouped[k] = {}
-            grouped[k][EVEN_LOW] = five_rounds.tile(
-                [P, CHUNK, PACK], BF16, name="even_low_words", align_bytes=64
-            )[:, columns(k), :]
+            grouped[k] = five_rounds.tile([P, 2, CHUNK, PACK], BF16, name="low_words", align_bytes=64)
+            words = grouped[k][:, EVEN_LOW, columns(k), :]
             nc.gpsimd.tensor_scalar(
-                out=words_in_the_same_order(grouped[k][EVEN_LOW]),
+                out=words_in_the_same_order(words),
                 in0=planes_in_word_order(even_low[k]),
                 scalar1=0.5,
                 scalar2=-1.0,
@@ -185,8 +183,19 @@ def tile_function_kernel(tc, x, w, out):
             shifted_product(odd_low[k][:, 2, :], five[k], 1.25, x_turned[k])
             shifted_product(odd_low[k][:, 1, :], even_low[k][:, 1, :], 3.0, x_turned[k])
 
-        def most_of_t7(k):
-            shifted_product(odd_low[k][:, 3, :], even_low[k][:, 2, :], 2.0, odd_low[k][:, 1, :])
+        def copy_some_of_s2_to_psum(k):
+            s2_copy[k] = s2_psum.tile([P, CHUNK], F32, name="s2_copy")[:, : fused(k)]
+            nc.tensor.matmul(
+                out=s2_copy[k], lhsT=identity_f32[:], rhs=even_low[k][:, 2, : fused(k)], start=True, stop=True
+            )
+
+        def most_of_t7_in_the_first_columns(k):
+            f = fused(k)
+            shifted_product(odd_low[k][:, 3, :f], s2_copy[k], 2.0, odd_low[k][:, 1, :f])
+
+        def most_of_t7_in_the_other_columns(k):
+            f = fused(k)
+            shifted_product(odd_low[k][:, 3, f:], even_low[k][:, 2, f:], 2.0, odd_low[k][:, 1, f:])
 
         def finish_t7(k):
             subtract(odd_low[k][:, 3, :], odd_low[k][:, 3, :], x_turned[k])
@@ -206,7 +215,10 @@ def tile_function_kernel(tc, x, w, out):
             square(even_high[k][:, 3, :], even_high[k][:, 0, :], 1.0, minus_two[:])
 
         def fused(k):
-            return CHUNK_TILES[k] * P * 5 // 8
+            return CHUNK_TILES[k] * P * FUSED // 32
+
+        def given(k):
+            return CHUNK_TILES[k] * P * GIVEN // 32
 
         def twice(plane):
             return plane.unsqueeze(1).to_broadcast([P, 2, plane.shape[-1]])
@@ -215,41 +227,47 @@ def tile_function_kernel(tc, x, w, out):
             odd_high[k] = two_rounds.tile([P, PACK, CHUNK], F32, name="odd_high")[:, :, columns(k)]
             shifted_product(odd_high[k][:, 2:4, :], twice(s3_copy[k]), 2.0, odd_low[k][:, 2:4, :])
 
-        def most_of_t9_and_t15(k):
+        def t9_or_most_of_it(k):
             f = fused(k)
-            shifted_product(
-                odd_high[k][:, 0:2, :f], even_low[k][:, 2:4, :f], 2.0, odd_low[k][:, 2:4, :f]
-            )
-            shifted_product(
-                odd_high[k][:, 0:2, f:], even_high[k][:, 0:2, f:], 3.0, odd_low[k][:, 1:3, f:]
-            )
+            shifted_product(odd_high[k][:, 0, f:], s3_copy[k][:, f:], 3.0, odd_low[k][:, 1, f:])
+            shifted_product(odd_high[k][:, 0, :f], s2_copy[k], 2.0, odd_low[k][:, 2, :f])
+
+        def t15_or_most_of_it(k):
+            f = fused(k)
+            shifted_product(odd_high[k][:, 1, :f], even_low[k][:, 3, :f], 2.0, odd_low[k][:, 3, :f])
+            shifted_product(odd_high[k][:, 1, f:], even_high[k][:, 1, f:], 3.0, odd_low[k][:, 2, f:])
 
         def finish_and_round_odd_high(k):
             f = fused(k)
-            grouped[k][ODD_HIGH] = two_rounds.tile(
-                [P, CHUNK, PACK], BF16, name="odd_high_words", align_bytes=64
-            )[:, columns(k), :]
             x_run = x_turned[k][:, :f].rearrange("p (c i) -> p c i", i=RUN).unsqueeze(2)
             subtract(
-                words_in_the_same_order(grouped[k][ODD_HIGH][:, :f, :]),
+                words_in_the_same_order(high_words[k][:, 1, :f, :]),
                 planes_in_word_order(odd_high[k][:, :, :f]),
                 x_run.to_broadcast([P, f // RUN, PACK, RUN]),
             )
             subtract(odd_high[k][:, 2:4, f:], odd_high[k][:, 2:4, f:], twice(x_turned[k][:, f:]))
 
+        def round_some_of_odd_high_on_gpsimd(k):
+            f, g = fused(k), fused(k) + given(k)
+            nc.gpsimd.tensor_scalar(
+                out=words_in_the_same_order(high_words[k][:, 1, f:g, :]),
+                in0=planes_in_word_order(odd_high[k][:, :, f:g]),
+                scalar1=1.0,
+                scalar2=0.0,
+                op0=ALU.mult,
+                op1=ALU.add,
+            )
+
         def round_the_rest_of_odd_high(k):
-            f = fused(k)
+            f = fused(k) + given(k)
             nc.scalar.copy(
-                out=words_in_the_same_order(grouped[k][ODD_HIGH][:, f:, :]),
+                out=words_in_the_same_order(high_words[k][:, 1, f : CHUNK_TILES[k] * P, :]),
                 in_=planes_in_word_order(odd_high[k][:, :, f:]),
             )
 
         def round_odd_low_on_gpsimd(k):
-            grouped[k][ODD_LOW] = three_rounds.tile(
-                [P, CHUNK, PACK], BF16, name="odd_low_words", align_bytes=64
-            )[:, columns(k), :]
             nc.gpsimd.tensor_scalar(
-                out=words_in_the_same_order(grouped[k][ODD_LOW]),
+                out=words_in_the_same_order(grouped[k][:, ODD_LOW, columns(k), :]),
                 in0=planes_in_word_order(odd_low[k]),
                 scalar1=1.0,
                 scalar2=0.0,
@@ -258,11 +276,9 @@ def tile_function_kernel(tc, x, w, out):
             )
 
         def round_even_high(k):
-            grouped[k][EVEN_HIGH] = three_rounds.tile(
-                [P, CHUNK, PACK], BF16, name="even_high_words", align_bytes=64
-            )[:, columns(k), :]
+            high_words[k] = three_rounds.tile([P, 2, CHUNK, PACK], BF16, name="high_words", align_bytes=64)
             nc.scalar.activation(
-                out=words_in_the_same_order(grouped[k][EVEN_HIGH]),
+                out=words_in_the_same_order(high_words[k][:, 0, columns(k), :]),
                 in_=planes_in_word_order(even_high[k]),
                 func=ACT.Identity,
                 scale=0.5,
@@ -272,12 +288,21 @@ def tile_function_kernel(tc, x, w, out):
         def quantise(k):
             codes[k] = two_rounds.tile([P, PASSES, CHUNK], U32, name="codes", align_bytes=64)
             scales[k] = two_rounds.tile([P, PASSES, CHUNK], U8, name="scales", align_bytes=64)
-            for c in range(PASSES):
-                nc.vector.quantize_mx(
-                    out=codes[k][:, c, columns(k)].bitcast(FP8X4),
-                    scales=scales[k][:, c, columns(k)],
-                    in_=grouped[k][c].rearrange("p w t -> p (w t)"),
-                )
+            for first_pass, words in ((0, grouped[k]), (2, high_words[k])):
+                if CHUNK_TILES[k] == FULL:
+                    two = slice(first_pass, first_pass + 2)
+                    nc.vector.quantize_mx(
+                        out=codes[k][:, two, :].rearrange("p c w -> p (c w)").bitcast(FP8X4),
+                        scales=scales[k][:, two, :].rearrange("p c w -> p (c w)"),
+                        in_=words[:].rearrange("p c w t -> p (c w t)"),
+                    )
+                else:
+                    for c in range(2):
+                        nc.vector.quantize_mx(
+                            out=codes[k][:, first_pass + c, columns(k)].bitcast(FP8X4),
+                            scales=scales[k][:, first_pass + c, columns(k)],
+                            in_=words[:, c, columns(k), :].rearrange("p w t -> p (w t)"),
+                        )
 
         def multiply(k):
             sums[k] = out_psum.tile([P, FULL, OUTPUTS], F32, name="sums")[:, : CHUNK_TILES[k], :]
@@ -304,8 +329,8 @@ def tile_function_kernel(tc, x, w, out):
             return 0 <= k < CHUNKS
 
         fetch(0)
-        fetch_weights()
         fetch(1)
+        fetch_weights()
         with tc.manual_schedule():
             for j in range(-3, CHUNKS + 3):
                 if is_chunk(j):
@@ -314,7 +339,10 @@ def tile_function_kernel(tc, x, w, out):
                     s7_and_s6(j)
                 if is_chunk(j - 1):
                     finish_and_round_odd_high(j - 1)
+                    round_some_of_odd_high_on_gpsimd(j - 1)
                     round_the_rest_of_odd_high(j - 1)
+                if is_chunk(j - 3):
+                    store(j - 3)
                 if is_chunk(j + 2):
                     squares_from_x(j + 2)
                     round_even_low_on_gpsimd(j + 2)
@@ -323,6 +351,9 @@ def tile_function_kernel(tc, x, w, out):
                     s3_and_s5(j + 1)
                 if is_chunk(j):
                     most_of_t11_and_t13(j)
+                    t9_or_most_of_it(j)
+                if is_chunk(j + 1):
+                    most_of_t7_in_the_first_columns(j + 1)
                 if is_chunk(j + 3):
                     if FIRST_TILE[j + 3] in PIECE_AT:
                         piece = PIECE_AT[FIRST_TILE[j + 3]]
@@ -332,20 +363,20 @@ def tile_function_kernel(tc, x, w, out):
                     turn(j + 3)
                 if is_chunk(j + 1):
                     copy_s3_to_psum(j + 1)
+                if is_chunk(j + 2):
+                    copy_some_of_s2_to_psum(j + 2)
                 if is_chunk(j):
-                    most_of_t9_and_t15(j)
+                    t15_or_most_of_it(j)
                 if is_chunk(j + 1):
-                    most_of_t7(j + 1)
+                    most_of_t7_in_the_other_columns(j + 1)
                 if is_chunk(j):
                     round_even_high(j)
-                if j == -2:
-                    turn_weights(0)
                 if j == -1:
-                    turn_weights(2)
+                    turn_weights(0)
                 if j == 0:
+                    turn_weights(2)
+                if j == 1:
                     quantise_weights()
                 if is_chunk(j - 2):
                     quantise(j - 2)
                     multiply(j - 2)
-                if is_chunk(j - 3):
-                    store(j - 3)

@@ -341,11 +341,11 @@ def tile_function_kernel(tc, x, w, out):
                     finish_and_round_odd_high(j - 1)
                     round_some_of_odd_high_on_gpsimd(j - 1)
                     round_the_rest_of_odd_high(j - 1)
-                if is_chunk(j - 3):
-                    store(j - 3)
                 if is_chunk(j + 2):
                     squares_from_x(j + 2)
                     round_even_low_on_gpsimd(j + 2)
+                if is_chunk(j - 3):
+                    store(j - 3)
                 if is_chunk(j + 1):
                     t5_and_t3(j + 1)
                     s3_and_s5(j + 1)
@@ -361,10 +361,10 @@ def tile_function_kernel(tc, x, w, out):
                             fetch(piece + 2)
                         sort_features(piece)
                     turn(j + 3)
-                if is_chunk(j + 1):
-                    copy_s3_to_psum(j + 1)
                 if is_chunk(j + 2):
                     copy_some_of_s2_to_psum(j + 2)
+                if is_chunk(j + 1):
+                    copy_s3_to_psum(j + 1)
                 if is_chunk(j):
                     t15_or_most_of_it(j)
                 if is_chunk(j + 1):

@@ -33,7 +33,7 @@ PIECES = ((0, slice(0, FULL)), (0, slice(FULL, LOAD_ROWS))) + tuple(
 PIECE_AT = {load * LOAD_ROWS + rows.start: piece for piece, (load, rows) in enumerate(PIECES)}
 RUN = 4
 
-FUSED, GIVEN = 18, 4
+FUSED, GIVEN = 12, 8
 
 FLOPS = 2 * BATCH * FEATURES * DEGREES * OUTPUTS
 
@@ -85,17 +85,18 @@ def tile_function_kernel(tc, x, w, out):
         loads = ctx.enter_context(tc.tile_pool(name="loads", bufs=3))
         three_rounds = ctx.enter_context(tc.tile_pool(name="three_rounds", bufs=3))
         two_rounds = ctx.enter_context(tc.tile_pool(name="two_rounds", bufs=2))
+        four_rounds = ctx.enter_context(tc.tile_pool(name="four_rounds", bufs=4))
         five_rounds = ctx.enter_context(tc.tile_pool(name="five_rounds", bufs=5))
         x_psum = ctx.enter_context(tc.psum_pool(name="x_psum", bufs=4))
-        s2_psum = ctx.enter_context(tc.psum_pool(name="s2_psum", bufs=2))
+        s2_psum = ctx.enter_context(tc.psum_pool(name="s2_psum", bufs=1))
         s3_psum = ctx.enter_context(tc.psum_pool(name="s3_psum", bufs=1))
-        out_psum = ctx.enter_context(tc.psum_pool(name="out_psum", bufs=1))
+        out_psum = ctx.enter_context(tc.psum_pool(name="out_psum", bufs=2))
 
         x_loads = x.rearrange("(l p r) f -> l p (r f)", p=P, r=LOAD_ROWS)
         out_loads = out.rearrange("(l p r) o -> l p r o", p=P, r=LOAD_ROWS)
 
         x_rows, x_sorted, x_turned = {}, {}, {}
-        even_low, odd_low, even_high, odd_high, five = {}, {}, {}, {}, {}
+        even_low, even_high, odd, five = {}, {}, {}, {}
         s2_copy, s3_copy, grouped, high_words, codes, scales, sums = {}, {}, {}, {}, {}, {}, {}
 
         w_codes = keep.tile([P, PASSES, OUTPUTS], U32, align_bytes=64)
@@ -158,11 +159,11 @@ def tile_function_kernel(tc, x, w, out):
 
         def squares_from_x(k):
             even_low[k] = even_low_planes[k % 3][:, :, columns(k)]
-            odd_low[k] = three_rounds.tile([P, PACK, CHUNK], F32, name="odd_low")[:, :, columns(k)]
+            odd[k] = four_rounds.tile([P, 2 * PACK, CHUNK], F32, name="odd")[:, :, columns(k)]
             five[k] = two_rounds.tile([P, CHUNK], F32, name="five")[:, columns(k)]
             s1, s2, s4 = (even_low[k][:, t, :] for t in range(1, PACK))
             square(s1, x_turned[k], 2.0)
-            nc.scalar.copy(out=odd_low[k][:, 0, :], in_=x_turned[k])
+            nc.scalar.copy(out=odd[k][:, 0, :], in_=x_turned[k])
             square(s2, s1, 1.0, minus_two[:])
             square(five[k], s1, 1.0, minus_five_halves[:])
             square(s4, s2, 1.0, minus_two[:])
@@ -180,8 +181,8 @@ def tile_function_kernel(tc, x, w, out):
             )
 
         def t5_and_t3(k):
-            shifted_product(odd_low[k][:, 2, :], five[k], 1.25, x_turned[k])
-            shifted_product(odd_low[k][:, 1, :], even_low[k][:, 1, :], 3.0, x_turned[k])
+            shifted_product(odd[k][:, 2, :], five[k], 1.25, x_turned[k])
+            shifted_product(odd[k][:, 1, :], even_low[k][:, 1, :], 3.0, x_turned[k])
 
         def copy_some_of_s2_to_psum(k):
             s2_copy[k] = s2_psum.tile([P, CHUNK], F32, name="s2_copy")[:, : fused(k)]
@@ -189,20 +190,20 @@ def tile_function_kernel(tc, x, w, out):
                 out=s2_copy[k], lhsT=identity_f32[:], rhs=even_low[k][:, 2, : fused(k)], start=True, stop=True
             )
 
-        def most_of_t7_in_the_first_columns(k):
+        def most_of_t7_and_t9_in_the_first_columns(k):
             f = fused(k)
-            shifted_product(odd_low[k][:, 3, :f], s2_copy[k], 2.0, odd_low[k][:, 1, :f])
+            shifted_product(odd[k][:, 3:5, :f], twice(s2_copy[k]), 2.0, odd[k][:, 1:3, :f])
 
         def most_of_t7_in_the_other_columns(k):
             f = fused(k)
-            shifted_product(odd_low[k][:, 3, f:], even_low[k][:, 2, f:], 2.0, odd_low[k][:, 1, f:])
+            shifted_product(odd[k][:, 3, f:], even_low[k][:, 2, f:], 2.0, odd[k][:, 1, f:])
 
         def finish_t7(k):
-            subtract(odd_low[k][:, 3, :], odd_low[k][:, 3, :], x_turned[k])
+            subtract(odd[k][:, 3, :], odd[k][:, 3, :], x_turned[k])
 
         def s3_and_s5(k):
             even_high[k] = two_rounds.tile([P, PACK, CHUNK], F32, name="even_high")[:, :, columns(k)]
-            square(even_high[k][:, 0:2, :], odd_low[k][:, 1:3, :], 2.0)
+            square(even_high[k][:, 0:2, :], odd[k][:, 1:3, :], 2.0)
 
         def copy_s3_to_psum(k):
             s3_copy[k] = s3_psum.tile([P, CHUNK], F32, name="s3_copy")[:, columns(k)]
@@ -211,7 +212,7 @@ def tile_function_kernel(tc, x, w, out):
             )
 
         def s7_and_s6(k):
-            square(even_high[k][:, 2, :], odd_low[k][:, 3, :], 2.0)
+            square(even_high[k][:, 2, :], odd[k][:, 3, :], 2.0)
             square(even_high[k][:, 3, :], even_high[k][:, 0, :], 1.0, minus_two[:])
 
         def fused(k):
@@ -224,34 +225,32 @@ def tile_function_kernel(tc, x, w, out):
             return plane.unsqueeze(1).to_broadcast([P, 2, plane.shape[-1]])
 
         def most_of_t11_and_t13(k):
-            odd_high[k] = two_rounds.tile([P, PACK, CHUNK], F32, name="odd_high")[:, :, columns(k)]
-            shifted_product(odd_high[k][:, 2:4, :], twice(s3_copy[k]), 2.0, odd_low[k][:, 2:4, :])
+            shifted_product(odd[k][:, 6:8, :], twice(s3_copy[k]), 2.0, odd[k][:, 2:4, :])
 
-        def t9_or_most_of_it(k):
+        def t9_in_the_other_columns(k):
             f = fused(k)
-            shifted_product(odd_high[k][:, 0, f:], s3_copy[k][:, f:], 3.0, odd_low[k][:, 1, f:])
-            shifted_product(odd_high[k][:, 0, :f], s2_copy[k], 2.0, odd_low[k][:, 2, :f])
+            shifted_product(odd[k][:, 4, f:], s3_copy[k][:, f:], 3.0, odd[k][:, 1, f:])
 
         def t15_or_most_of_it(k):
             f = fused(k)
-            shifted_product(odd_high[k][:, 1, :f], even_low[k][:, 3, :f], 2.0, odd_low[k][:, 3, :f])
-            shifted_product(odd_high[k][:, 1, f:], even_high[k][:, 1, f:], 3.0, odd_low[k][:, 2, f:])
+            shifted_product(odd[k][:, 5, :f], even_low[k][:, 3, :f], 2.0, odd[k][:, 3, :f])
+            shifted_product(odd[k][:, 5, f:], even_high[k][:, 1, f:], 3.0, odd[k][:, 2, f:])
 
         def finish_and_round_odd_high(k):
             f = fused(k)
             x_run = x_turned[k][:, :f].rearrange("p (c i) -> p c i", i=RUN).unsqueeze(2)
             subtract(
                 words_in_the_same_order(high_words[k][:, 1, :f, :]),
-                planes_in_word_order(odd_high[k][:, :, :f]),
+                planes_in_word_order(odd[k][:, PACK:, :f]),
                 x_run.to_broadcast([P, f // RUN, PACK, RUN]),
             )
-            subtract(odd_high[k][:, 2:4, f:], odd_high[k][:, 2:4, f:], twice(x_turned[k][:, f:]))
+            subtract(odd[k][:, 6:8, f:], odd[k][:, 6:8, f:], twice(x_turned[k][:, f:]))
 
         def round_some_of_odd_high_on_gpsimd(k):
             f, g = fused(k), fused(k) + given(k)
             nc.gpsimd.tensor_scalar(
                 out=words_in_the_same_order(high_words[k][:, 1, f:g, :]),
-                in0=planes_in_word_order(odd_high[k][:, :, f:g]),
+                in0=planes_in_word_order(odd[k][:, PACK:, f:g]),
                 scalar1=1.0,
                 scalar2=0.0,
                 op0=ALU.mult,
@@ -262,13 +261,13 @@ def tile_function_kernel(tc, x, w, out):
             f = fused(k) + given(k)
             nc.scalar.copy(
                 out=words_in_the_same_order(high_words[k][:, 1, f : CHUNK_TILES[k] * P, :]),
-                in_=planes_in_word_order(odd_high[k][:, :, f:]),
+                in_=planes_in_word_order(odd[k][:, PACK:, f:]),
             )
 
         def round_odd_low_on_gpsimd(k):
             nc.gpsimd.tensor_scalar(
                 out=words_in_the_same_order(grouped[k][:, ODD_LOW, columns(k), :]),
-                in0=planes_in_word_order(odd_low[k]),
+                in0=planes_in_word_order(odd[k][:, :PACK, :]),
                 scalar1=1.0,
                 scalar2=0.0,
                 op0=ALU.mult,
@@ -351,9 +350,9 @@ def tile_function_kernel(tc, x, w, out):
                     s3_and_s5(j + 1)
                 if is_chunk(j):
                     most_of_t11_and_t13(j)
-                    t9_or_most_of_it(j)
+                    t9_in_the_other_columns(j)
                 if is_chunk(j + 1):
-                    most_of_t7_in_the_first_columns(j + 1)
+                    most_of_t7_and_t9_in_the_first_columns(j + 1)
                 if is_chunk(j + 3):
                     if FIRST_TILE[j + 3] in PIECE_AT:
                         piece = PIECE_AT[FIRST_TILE[j + 3]]

@@ -33,7 +33,7 @@ PIECES = ((0, slice(0, FULL)), (0, slice(FULL, LOAD_ROWS))) + tuple(
 PIECE_AT = {load * LOAD_ROWS + rows.start: piece for piece, (load, rows) in enumerate(PIECES)}
 RUN = 4
 
-FUSED, GIVEN = 12, 8
+FUSED, GIVEN = 18, 4
 
 FLOPS = 2 * BATCH * FEATURES * DEGREES * OUTPUTS
 
@@ -89,8 +89,8 @@ def tile_function_kernel(tc, x, w, out):
         five_rounds = ctx.enter_context(tc.tile_pool(name="five_rounds", bufs=5))
         x_psum = ctx.enter_context(tc.psum_pool(name="x_psum", bufs=4))
         s2_psum = ctx.enter_context(tc.psum_pool(name="s2_psum", bufs=1))
-        s3_psum = ctx.enter_context(tc.psum_pool(name="s3_psum", bufs=1))
-        out_psum = ctx.enter_context(tc.psum_pool(name="out_psum", bufs=2))
+        s3_psum = ctx.enter_context(tc.psum_pool(name="s3_psum", bufs=2))
+        out_psum = ctx.enter_context(tc.psum_pool(name="out_psum", bufs=1))
 
         x_loads = x.rearrange("(l p r) f -> l p (r f)", p=P, r=LOAD_ROWS)
         out_loads = out.rearrange("(l p r) o -> l p r o", p=P, r=LOAD_ROWS)
@@ -102,20 +102,23 @@ def tile_function_kernel(tc, x, w, out):
         w_codes = keep.tile([P, PASSES, OUTPUTS], U32, align_bytes=64)
         w_scales = keep.tile([P, PASSES, OUTPUTS], U8, align_bytes=64)
         w_rows = stage.tile([P, FEATURES * DEGREES], BF16)
+        w_sorted = stage.tile([P, FEATURES * DEGREES], BF16)
         w_grouped = stage.tile([P, PASSES, OUTPUTS, PACK], BF16, align_bytes=64)
 
         def fetch_weights():
-            w_pairs = w.rearrange("o (g s q e) n -> o g q s (e n)", g=4, s=4, q=4, e=2)
-            sorted_pairs = w_rows[:].rearrange("o (g q s m) -> o g q s m", g=4, q=4, s=4)
-            for g in range(4):
-                for q in range(4):
-                    nc.sync.dma_start(out=sorted_pairs[:, g, q], in_=w_pairs[:, g, q])
+            nc.sync.dma_start(out=w_rows[:], in_=w.rearrange("o i n -> o (i n)"))
+
+        def sort_weights():
+            nc.vector.tensor_copy(
+                out=w_sorted[:].bitcast(F32).rearrange("o (g q s m) -> o g q s m", g=4, q=4, s=4),
+                in_=w_rows[:].bitcast(F32).rearrange("o (g s q m) -> o g q s m", g=4, q=4, s=4),
+            )
 
         def turn_weights(first_pass):
             w_turned = out_psum.tile([P, 2 * PACK, OUTPUTS], BF16, tag="sums")
             for k in range(2 * PACK):
                 degree = WORD_DEGREES[first_pass + k // PACK][k % PACK]
-                nc.tensor.transpose(w_turned[:, k, :], w_rows[:, degree : FEATURES * DEGREES : DEGREES], identity[:])
+                nc.tensor.transpose(w_turned[:, k, :], w_sorted[:, degree : FEATURES * DEGREES : DEGREES], identity[:])
             nc.scalar.copy(
                 out=w_grouped[:, first_pass : first_pass + 2, :, :],
                 in_=w_turned[:].rearrange("p (c t) o -> p c o t", t=PACK),
@@ -135,12 +138,13 @@ def tile_function_kernel(tc, x, w, out):
             load, rows = PIECES[piece]
             if rows.start == 0:
                 x_rows[load] = loads.tile([P, LOAD_ROWS * FEATURES], BF16, name="x_rows")
-                x_sorted[load] = loads.tile([P, LOAD_ROWS * FEATURES], BF16, name="x_sorted")
             part = slice(rows.start * FEATURES, rows.stop * FEATURES)
             nc.sync.dma_start(out=x_rows[load][:, part], in_=x_loads[load][:, part])
 
         def sort_features(piece):
             load, rows = PIECES[piece]
+            if rows.start == 0:
+                x_sorted[load] = two_rounds.tile([P, LOAD_ROWS * FEATURES], BF16, name="x_sorted")
             part = slice(rows.start * FEATURES, rows.stop * FEATURES)
             nc.vector.tensor_copy(
                 out=x_sorted[load][:, part].bitcast(F32).rearrange("p (a q s) -> p a q s", q=4, s=4),
@@ -328,31 +332,33 @@ def tile_function_kernel(tc, x, w, out):
             return 0 <= k < CHUNKS
 
         fetch(0)
-        fetch(1)
         fetch_weights()
+        fetch(1)
         with tc.manual_schedule():
             for j in range(-3, CHUNKS + 3):
                 if is_chunk(j):
                     finish_t7(j)
                     round_odd_low_on_gpsimd(j)
                     s7_and_s6(j)
+                if is_chunk(j + 1):
+                    t5_and_t3(j + 1)
+                    s3_and_s5(j + 1)
+                    copy_s3_to_psum(j + 1)
                 if is_chunk(j - 1):
                     finish_and_round_odd_high(j - 1)
                     round_some_of_odd_high_on_gpsimd(j - 1)
-                    round_the_rest_of_odd_high(j - 1)
                 if is_chunk(j + 2):
                     squares_from_x(j + 2)
                     round_even_low_on_gpsimd(j + 2)
                 if is_chunk(j - 3):
                     store(j - 3)
+                if is_chunk(j - 1):
+                    round_the_rest_of_odd_high(j - 1)
                 if is_chunk(j + 1):
-                    t5_and_t3(j + 1)
-                    s3_and_s5(j + 1)
+                    most_of_t7_and_t9_in_the_first_columns(j + 1)
                 if is_chunk(j):
                     most_of_t11_and_t13(j)
                     t9_in_the_other_columns(j)
-                if is_chunk(j + 1):
-                    most_of_t7_and_t9_in_the_first_columns(j + 1)
                 if is_chunk(j + 3):
                     if FIRST_TILE[j + 3] in PIECE_AT:
                         piece = PIECE_AT[FIRST_TILE[j + 3]]
@@ -362,14 +368,14 @@ def tile_function_kernel(tc, x, w, out):
                     turn(j + 3)
                 if is_chunk(j + 2):
                     copy_some_of_s2_to_psum(j + 2)
-                if is_chunk(j + 1):
-                    copy_s3_to_psum(j + 1)
                 if is_chunk(j):
                     t15_or_most_of_it(j)
                 if is_chunk(j + 1):
                     most_of_t7_in_the_other_columns(j + 1)
                 if is_chunk(j):
                     round_even_high(j)
+                if j == -2:
+                    sort_weights()
                 if j == -1:
                     turn_weights(0)
                 if j == 0:

@@ -33,7 +33,8 @@ PIECES = ((0, slice(0, FULL)), (0, slice(FULL, LOAD_ROWS))) + tuple(
 PIECE_AT = {load * LOAD_ROWS + rows.start: piece for piece, (load, rows) in enumerate(PIECES)}
 RUN = 4
 
-FUSED, GIVEN = 18, 4
+FUSED, GIVEN = 16, 4
+FUSED_AT_THE_END, LAST_CHUNKS = 8, 6
 
 FLOPS = 2 * BATCH * FEATURES * DEGREES * OUTPUTS
 
@@ -220,7 +221,8 @@ def tile_function_kernel(tc, x, w, out):
             square(even_high[k][:, 3, :], even_high[k][:, 0, :], 1.0, minus_two[:])
 
         def fused(k):
-            return CHUNK_TILES[k] * P * FUSED // 32
+            share = FUSED if k < CHUNKS - LAST_CHUNKS else FUSED_AT_THE_END
+            return CHUNK_TILES[k] * P * share // 32
 
         def given(k):
             return CHUNK_TILES[k] * P * GIVEN // 32

from contextlib import ExitStack

import concourse.mybir as mybir
from concourse.masks import make_identity

F32 = mybir.dt.float32
BF16 = mybir.dt.bfloat16
U32 = mybir.dt.uint32
U8 = mybir.dt.uint8
FP8X4 = mybir.dt.float8_e4m3fn_x4
ALU = mybir.AluOpType
ACT = mybir.ActivationFunctionType

P = 128
PACK = 4
BATCH, FEATURES, OUTPUTS, DEGREES = 16384, 128, 128, 16
PASSES = DEGREES // PACK

WORD_DEGREES = ((0, 2, 4, 8), (1, 3, 5, 7), (6, 10, 14, 12), (9, 15, 11, 13))
EVEN_LOW, ODD_LOW, EVEN_HIGH, ODD_HIGH = 0, 1, 2, 3

CHUNK = 512
LOAD_ROWS = 16
LOADS = BATCH // (P * LOAD_ROWS)
RAMP_UP, RAMP_DOWN = (1, 1, 2), (2, 1, 1)
FULL = CHUNK // P
CHUNK_TILES = RAMP_UP + (FULL,) * ((BATCH // P - sum(RAMP_UP + RAMP_DOWN)) // FULL) + RAMP_DOWN
CHUNKS = len(CHUNK_TILES)
FIRST_TILE = tuple(sum(CHUNK_TILES[:k]) for k in range(CHUNKS))
PIECES = ((0, slice(0, FULL)), (0, slice(FULL, LOAD_ROWS))) + tuple(
    (load, slice(0, LOAD_ROWS)) for load in range(1, LOADS)
)
PIECE_AT = {load * LOAD_ROWS + rows.start: piece for piece, (load, rows) in enumerate(PIECES)}
RUN = 4

FUSED, GIVEN = 16, 4
FUSED_AT_THE_END, LAST_CHUNKS = 8, 6

FLOPS = 2 * BATCH * FEATURES * DEGREES * OUTPUTS


def planes_in_word_order(planes):
    return planes.rearrange("p t (c i) -> p c t i", i=RUN)


def words_in_the_same_order(grouped):
    return grouped.rearrange("p (c i) t -> p c t i", i=RUN)


def tile_function_kernel(tc, x, w, out):
    nc = tc.nc

    def square(out_plane, in_plane, scale, bias=None):
        if bias is None:
            nc.scalar.activation(out=out_plane, in_=in_plane, func=ACT.Square, scale=scale)
        else:
            nc.scalar.activation(out=out_plane, in_=in_plane, func=ACT.Square, scale=scale, bias=bias)

    def shifted_product(out_plane, a, shift, b):
        nc.vector.scalar_tensor_tensor(
            out=out_plane, in0=a, scalar=shift, in1=b, op0=ALU.subtract, op1=ALU.mult
        )

    def subtract(out_plane, a, b):
        nc.vector.tensor_tensor(out=out_plane, in0=a, in1=b, op=ALU.subtract)

    with ExitStack() as ctx:
        keep = ctx.enter_context(tc.tile_pool(name="keep", bufs=1))
        identity = keep.tile([P, P], BF16)
        make_identity(nc, identity[:])
        identity_f32 = keep.tile([P, P], F32)
        make_identity(nc, identity_f32[:])
        minus_one = keep.tile([P, 1], F32)
        minus_two = keep.tile([P, 1], F32)
        minus_five_halves = keep.tile([P, 1], F32)
        nc.vector.memset(minus_one[:], -1.0)
        nc.vector.memset(minus_two[:], -2.0)
        nc.vector.memset(minus_five_halves[:], -2.5)
        even_low_planes = []
        for k in range(3):
            fixed = keep.tile([P, PACK, CHUNK], F32, name="even_low_planes_%d" % k)
            nc.gpsimd.memset(fixed[:, 0, :], 4.0)
            even_low_planes.append(fixed)

        stage = ctx.enter_context(tc.tile_pool(name="w_stage", bufs=1))
        loads = ctx.enter_context(tc.tile_pool(name="loads", bufs=3))
        three_rounds = ctx.enter_context(tc.tile_pool(name="three_rounds", bufs=3))
        two_rounds = ctx.enter_context(tc.tile_pool(name="two_rounds", bufs=2))
        four_rounds = ctx.enter_context(tc.tile_pool(name="four_rounds", bufs=4))
        five_rounds = ctx.enter_context(tc.tile_pool(name="five_rounds", bufs=5))
        x_psum = ctx.enter_context(tc.psum_pool(name="x_psum", bufs=4))
        s2_psum = ctx.enter_context(tc.psum_pool(name="s2_psum", bufs=1))
        s3_psum = ctx.enter_context(tc.psum_pool(name="s3_psum", bufs=2))
        out_psum = ctx.enter_context(tc.psum_pool(name="out_psum", bufs=1))

        x_loads = x.rearrange("(l p r) f -> l p (r f)", p=P, r=LOAD_ROWS)
        out_loads = out.rearrange("(l p r) o -> l p r o", p=P, r=LOAD_ROWS)

        x_rows, x_sorted, x_turned = {}, {}, {}
        even_low, even_high, odd, five = {}, {}, {}, {}
        s2_copy, s3_copy, grouped, high_words, codes, scales, sums = {}, {}, {}, {}, {}, {}, {}

        w_codes = keep.tile([P, PASSES, OUTPUTS], U32, align_bytes=64)
        w_scales = keep.tile([P, PASSES, OUTPUTS], U8, align_bytes=64)
        w_rows = stage.tile([P, FEATURES * DEGREES], BF16)
        w_sorted = stage.tile([P, FEATURES * DEGREES], BF16)
        w_grouped = stage.tile([P, PASSES, OUTPUTS, PACK], BF16, align_bytes=64)

        def fetch_weights():
            nc.sync.dma_start(out=w_rows[:], in_=w.rearrange("o i n -> o (i n)"))

        def sort_weights():
            nc.vector.tensor_copy(
                out=w_sorted[:].bitcast(F32).rearrange("o (g q s m) -> o g q s m", g=4, q=4, s=4),
                in_=w_rows[:].bitcast(F32).rearrange("o (g s q m) -> o g q s m", g=4, q=4, s=4),
            )

        def turn_weights(first_pass):
            w_turned = out_psum.tile([P, 2 * PACK, OUTPUTS], BF16, tag="sums")
            for k in range(2 * PACK):
                degree = WORD_DEGREES[first_pass + k // PACK][k % PACK]
                nc.tensor.transpose(w_turned[:, k, :], w_sorted[:, degree : FEATURES * DEGREES : DEGREES], identity[:])
            nc.scalar.copy(
                out=w_grouped[:, first_pass : first_pass + 2, :, :],
                in_=w_turned[:].rearrange("p (c t) o -> p c o t", t=PACK),
            )

        def quantise_weights():
            nc.vector.quantize_mx(
                out=w_codes[:].rearrange("p c o -> p (c o)").bitcast(FP8X4),
                scales=w_scales[:].rearrange("p c o -> p (c o)"),
                in_=w_grouped[:].rearrange("p c o t -> p (c o t)"),
            )

        def columns(k):
            return slice(0, CHUNK_TILES[k] * P)

        def fetch(piece):
            load, rows = PIECES[piece]
            if rows.start == 0:
                x_rows[load] = loads.tile([P, LOAD_ROWS * FEATURES], BF16, name="x_rows")
            part = slice(rows.start * FEATURES, rows.stop * FEATURES)
            nc.sync.dma_start(out=x_rows[load][:, part], in_=x_loads[load][:, part])

        def sort_features(piece):
            load, rows = PIECES[piece]
            if rows.start == 0:
                x_sorted[load] = two_rounds.tile([P, LOAD_ROWS * FEATURES], BF16, name="x_sorted")
            part = slice(rows.start * FEATURES, rows.stop * FEATURES)
            nc.vector.tensor_copy(
                out=x_sorted[load][:, part].bitcast(F32).rearrange("p (a q s) -> p a q s", q=4, s=4),
                in_=x_rows[load][:, part].bitcast(F32).rearrange("p (a s q) -> p a q s", q=4, s=4),
            )

        def turn(k):
            x_turned[k] = x_psum.tile([P, CHUNK], BF16, name="x_turned")[:, columns(k)]
            for r in range(CHUNK_TILES[k]):
                load, row = divmod(FIRST_TILE[k] + r, LOAD_ROWS)
                nc.tensor.transpose(
                    x_turned[k][:, r * P : (r + 1) * P],
                    x_sorted[load][:, row * FEATURES : (row + 1) * FEATURES],
                    identity[:],
                )

        def squares_from_x(k):
            even_low[k] = even_low_planes[k % 3][:, :, columns(k)]
            odd[k] = four_rounds.tile([P, 2 * PACK, CHUNK], F32, name="odd")[:, :, columns(k)]
            five[k] = two_rounds.tile([P, CHUNK], F32, name="five")[:, columns(k)]
            s1, s2, s4 = (even_low[k][:, t, :] for t in range(1, PACK))
            square(s1, x_turned[k], 2.0)
            nc.scalar.copy(out=odd[k][:, 0, :], in_=x_turned[k])
            square(s2, s1, 1.0, minus_two[:])
            square(five[k], s1, 1.0, minus_five_halves[:])
            square(s4, s2, 1.0, minus_two[:])

        def round_even_low_on_gpsimd(k):
            grouped[k] = five_rounds.tile([P, 2, CHUNK, PACK], BF16, name="low_words", align_bytes=64)
            words = grouped[k][:, EVEN_LOW, columns(k), :]
            nc.gpsimd.tensor_scalar(
                out=words_in_the_same_order(words),
                in0=planes_in_word_order(even_low[k]),
                scalar1=0.5,
                scalar2=-1.0,
                op0=ALU.mult,
                op1=ALU.add,
            )

        def t5_and_t3(k):
            shifted_product(odd[k][:, 2, :], five[k], 1.25, x_turned[k])
            shifted_product(odd[k][:, 1, :], even_low[k][:, 1, :], 3.0, x_turned[k])

        def copy_some_of_s2_to_psum(k):
            s2_copy[k] = s2_psum.tile([P, CHUNK], F32, name="s2_copy")[:, : fused(k)]
            nc.tensor.matmul(
                out=s2_copy[k], lhsT=identity_f32[:], rhs=even_low[k][:, 2, : fused(k)], start=True, stop=True
            )

        def most_of_t7_and_t9_in_the_first_columns(k):
            f = fused(k)
            shifted_product(odd[k][:, 3:5, :f], twice(s2_copy[k]), 2.0, odd[k][:, 1:3, :f])

        def most_of_t7_in_the_other_columns(k):
            f = fused(k)
            shifted_product(odd[k][:, 3, f:], even_low[k][:, 2, f:], 2.0, odd[k][:, 1, f:])

        def finish_t7(k):
            subtract(odd[k][:, 3, :], odd[k][:, 3, :], x_turned[k])

        def s3_and_s5(k):
            even_high[k] = two_rounds.tile([P, PACK, CHUNK], F32, name="even_high")[:, :, columns(k)]
            square(even_high[k][:, 0:2, :], odd[k][:, 1:3, :], 2.0)

        def copy_s3_to_psum(k):
            s3_copy[k] = s3_psum.tile([P, CHUNK], F32, name="s3_copy")[:, columns(k)]
            nc.tensor.matmul(
                out=s3_copy[k], lhsT=identity_f32[:], rhs=even_high[k][:, 0, :], start=True, stop=True
            )

        def s7_and_s6(k):
            square(even_high[k][:, 2, :], odd[k][:, 3, :], 2.0)
            square(even_high[k][:, 3, :], even_high[k][:, 0, :], 1.0, minus_two[:])

        def fused(k):
            share = FUSED if k < CHUNKS - LAST_CHUNKS else FUSED_AT_THE_END
            return CHUNK_TILES[k] * P * share // 32

        def given(k):
            return CHUNK_TILES[k] * P * GIVEN // 32

        def twice(plane):
            return plane.unsqueeze(1).to_broadcast([P, 2, plane.shape[-1]])

        def most_of_t11_and_t13(k):
            shifted_product(odd[k][:, 6:8, :], twice(s3_copy[k]), 2.0, odd[k][:, 2:4, :])

        def t9_in_the_other_columns(k):
            f = fused(k)
            shifted_product(odd[k][:, 4, f:], s3_copy[k][:, f:], 3.0, odd[k][:, 1, f:])

        def t15_or_most_of_it(k):
            f = fused(k)
            shifted_product(odd[k][:, 5, :f], even_low[k][:, 3, :f], 2.0, odd[k][:, 3, :f])
            shifted_product(odd[k][:, 5, f:], even_high[k][:, 1, f:], 3.0, odd[k][:, 2, f:])

        def finish_and_round_odd_high(k):
            f = fused(k)
            x_run = x_turned[k][:, :f].rearrange("p (c i) -> p c i", i=RUN).unsqueeze(2)
            subtract(
                words_in_the_same_order(high_words[k][:, 1, :f, :]),
                planes_in_word_order(odd[k][:, PACK:, :f]),
                x_run.to_broadcast([P, f // RUN, PACK, RUN]),
            )
            subtract(odd[k][:, 6:8, f:], odd[k][:, 6:8, f:], twice(x_turned[k][:, f:]))

        def round_some_of_odd_high_on_gpsimd(k):
            f, g = fused(k), fused(k) + given(k)
            nc.gpsimd.tensor_scalar(
                out=words_in_the_same_order(high_words[k][:, 1, f:g, :]),
                in0=planes_in_word_order(odd[k][:, PACK:, f:g]),
                scalar1=1.0,
                scalar2=0.0,
                op0=ALU.mult,
                op1=ALU.add,
            )

        def round_the_rest_of_odd_high(k):
            f = fused(k) + given(k)
            nc.scalar.copy(
                out=words_in_the_same_order(high_words[k][:, 1, f : CHUNK_TILES[k] * P, :]),
                in_=planes_in_word_order(odd[k][:, PACK:, f:]),
            )

        def round_odd_low_on_gpsimd(k):
            nc.gpsimd.tensor_scalar(
                out=words_in_the_same_order(grouped[k][:, ODD_LOW, columns(k), :]),
                in0=planes_in_word_order(odd[k][:, :PACK, :]),
                scalar1=1.0,
                scalar2=0.0,
                op0=ALU.mult,
                op1=ALU.add,
            )

        def round_even_high(k):
            high_words[k] = three_rounds.tile([P, 2, CHUNK, PACK], BF16, name="high_words", align_bytes=64)
            nc.scalar.activation(
                out=words_in_the_same_order(high_words[k][:, 0, columns(k), :]),
                in_=planes_in_word_order(even_high[k]),
                func=ACT.Identity,
                scale=0.5,
                bias=minus_one[:],
            )

        def quantise(k):
            codes[k] = two_rounds.tile([P, PASSES, CHUNK], U32, name="codes", align_bytes=64)
            scales[k] = two_rounds.tile([P, PASSES, CHUNK], U8, name="scales", align_bytes=64)
            for first_pass, words in ((0, grouped[k]), (2, high_words[k])):
                if CHUNK_TILES[k] == FULL:
                    two = slice(first_pass, first_pass + 2)
                    nc.vector.quantize_mx(
                        out=codes[k][:, two, :].rearrange("p c w -> p (c w)").bitcast(FP8X4),
                        scales=scales[k][:, two, :].rearrange("p c w -> p (c w)"),
                        in_=words[:].rearrange("p c w t -> p (c w t)"),
                    )
                else:
                    for c in range(2):
                        nc.vector.quantize_mx(
                            out=codes[k][:, first_pass + c, columns(k)].bitcast(FP8X4),
                            scales=scales[k][:, first_pass + c, columns(k)],
                            in_=words[:, c, columns(k), :].rearrange("p w t -> p (w t)"),
                        )

        def multiply(k):
            sums[k] = out_psum.tile([P, FULL, OUTPUTS], F32, name="sums")[:, : CHUNK_TILES[k], :]
            for r in range(CHUNK_TILES[k]):
                tile_columns = slice(r * P, (r + 1) * P)
                for c in range(PASSES):
                    nc.tensor.matmul_mx(
                        out=sums[k][:, r, :],
                        lhsT=codes[k][:, c, tile_columns].bitcast(FP8X4),
                        lhsT_scale=scales[k][:, c, tile_columns],
                        rhs=w_codes[:, c, :].bitcast(FP8X4),
                        rhs_scale=w_scales[:, c, :],
                        start=(c == 0),
                        stop=(c == PASSES - 1),
                    )

        def store(k):
            result = three_rounds.tile([P, FULL, OUTPUTS], F32, name="result")[:, : CHUNK_TILES[k], :]
            nc.scalar.copy(out=result, in_=sums[k])
            load, row = divmod(FIRST_TILE[k], LOAD_ROWS)
            nc.sync.dma_start(out=out_loads[load][:, row : row + CHUNK_TILES[k], :], in_=result)

        def is_chunk(k):
            return 0 <= k < CHUNKS

        fetch(0)
        fetch_weights()
        fetch(1)
        with tc.manual_schedule():
            for j in range(-3, CHUNKS + 3):
                if is_chunk(j):
                    finish_t7(j)
                    round_odd_low_on_gpsimd(j)
                    s7_and_s6(j)
                if is_chunk(j + 1):
                    t5_and_t3(j + 1)
                    s3_and_s5(j + 1)
                    copy_s3_to_psum(j + 1)
                if is_chunk(j - 1):
                    finish_and_round_odd_high(j - 1)
                    round_some_of_odd_high_on_gpsimd(j - 1)
                if is_chunk(j + 2):
                    squares_from_x(j + 2)
                    round_even_low_on_gpsimd(j + 2)
                if is_chunk(j - 3):
                    store(j - 3)
                if is_chunk(j - 1):
                    round_the_rest_of_odd_high(j - 1)
                if is_chunk(j + 1):
                    most_of_t7_and_t9_in_the_first_columns(j + 1)
                if is_chunk(j):
                    most_of_t11_and_t13(j)
                    t9_in_the_other_columns(j)
                if is_chunk(j + 3):
                    if FIRST_TILE[j + 3] in PIECE_AT:
                        piece = PIECE_AT[FIRST_TILE[j + 3]]
                        if piece + 2 < len(PIECES):
                            fetch(piece + 2)
                        sort_features(piece)
                    turn(j + 3)
                if is_chunk(j + 2):
                    copy_some_of_s2_to_psum(j + 2)
                if is_chunk(j):
                    t15_or_most_of_it(j)
                if is_chunk(j + 1):
                    most_of_t7_in_the_other_columns(j + 1)
                if is_chunk(j):
                    round_even_high(j)
                if j == -2:
                    sort_weights()
                if j == -1:
                    turn_weights(0)
                if j == 0:
                    turn_weights(2)
                if j == 1:
                    quantise_weights()
                if is_chunk(j - 2):
                    quantise(j - 2)
                    multiply(j - 2)
